import numpy as np
import ml_dtypes


def mxq(x, axis, fmt="e4m3"):
    dtype, down = {"e4m3": (ml_dtypes.float8_e4m3fn, 7), "e5m2": (ml_dtypes.float8_e5m2, 14)}[fmt]
    v = np.moveaxis(np.asarray(x, np.float32).astype(ml_dtypes.bfloat16).astype(np.float64), axis, -1)
    blocks = v.reshape(v.shape[:-1] + (-1, 32))
    amax = np.abs(blocks).max(-1, keepdims=True)
    byte = np.maximum(np.where(amax > 0, np.frexp(amax)[1] - 1 + 127, 0) - down, 1)
    scale = np.exp2(byte - 127.0)
    codes = (blocks / scale).astype(np.float32).astype(dtype).astype(np.float64)
    return np.moveaxis((codes * scale).reshape(v.shape), -1, axis)


WIDE = False


def mx_kscale(k):
    if not WIDE:
        return np.ones(k)
    levels = np.array([10, -10, 5, -5, 0])
    a = np.random.permutation(np.resize(levels, k // 512 * 4)).reshape(k // 512, 4)
    idx = np.arange(k)
    return np.exp2(a[idx // 512, idx % 128 // 32])


BF16 = ml_dtypes.bfloat16


def bf(x):
    return np.asarray(x, np.float32).astype(BF16)


def f64(x):
    return np.asarray(x).astype(np.float64)


E2M1 = np.array([0.0, 0.5, 1.0, 1.5, 2.0, 3.0, 4.0, 6.0, -0.0, -0.5, -1.0, -1.5, -2.0, -3.0, -4.0, -6.0])


def pack_weight(w, fmt):
    k, n = w.shape
    w = f64(bf(w)).reshape(k // 32, 32, n)
    amax = np.abs(w).max(1)
    if fmt == "e4m3":
        byte = np.frexp(amax)[1] - 1 + 127 - 7
    else:
        mant, ex = np.frexp(amax / 6.0)
        byte = np.where(mant > 0.5, ex, ex - 1) + 127
    byte = np.clip(np.where(amax > 0, byte, 1), 1, 254)
    scaled = (w * np.exp2(127.0 - byte)[:, None, :]).reshape(k, n).astype(np.float32)
    by_word = np.ascontiguousarray(scaled.reshape(k // 512, 128, 4, n).transpose(0, 1, 3, 2))
    if fmt == "e4m3":
        words = by_word.astype(ml_dtypes.float8_e4m3fn).view(np.uint8)
    else:
        c = by_word.astype(ml_dtypes.float4_e2m1fn).view(np.uint8) & 0xF
        words = c[..., 0::2] | (c[..., 1::2] << 4)
    return np.ascontiguousarray(words), np.ascontiguousarray(byte.astype(np.uint8).reshape(k // 512, 16, n))


def unpack_weight(words, scales, fmt):
    g, p, n, _ = words.shape
    if fmt == "e4m3":
        vals = np.ascontiguousarray(words).view(ml_dtypes.float8_e4m3fn).astype(np.float64)
    else:
        nib = np.empty((g, p, n, 4), np.uint8)
        nib[..., 0::2] = words & 0xF
        nib[..., 1::2] = words >> 4
        vals = E2M1[nib]
    vals = vals * np.repeat(np.exp2(scales.astype(np.float64) - 127.0), 8, axis=1)[..., None]
    return vals.transpose(0, 1, 3, 2).reshape(g * 512, n)


L, F, O, N, B, D = 2, 512, 512, 1024, 1, 3
G = O + O + O


def sigmoid(v):
    return 1.0 / (1.0 + np.exp(-v))


def setup_inputs():
    s = mx_kscale(O)
    agg = bf(np.random.standard_normal((D, B, N, O)) * s)
    x = bf(np.random.standard_normal((N, B, F)))
    wih_words, wih_scales = pack_weight(np.ascontiguousarray((np.random.standard_normal((G, O)) * 0.7 / np.sqrt(O) / s).T), "e4m3")
    whh_words, whh_scales = pack_weight(np.ascontiguousarray((np.random.standard_normal((G, O)) * 0.7 / np.sqrt(O)).T), "e4m3")
    bih = bf(np.random.standard_normal(G) * 0.3)
    bhh = bf(np.random.standard_normal(G) * 0.3)
    wh_words, wh_scales = pack_weight(np.random.standard_normal((F, O)) * 0.5 / np.sqrt(F), "e4m3")
    bh = bf(0.3 + np.random.standard_normal(O) * 0.2)
    return {"agg": agg,
            "x": x,
            "wih_words": wih_words,
            "wih_scales": wih_scales,
            "whh_words": whh_words,
            "whh_scales": whh_scales,
            "bih": bih,
            "bhh": bhh,
            "wh_words": wh_words,
            "wh_scales": wh_scales,
            "bh": bh}


def reference(agg, x, wih_words, wih_scales, whh_words, whh_scales, bih, bhh, wh_words, wh_scales, bh):
    x = f64(x)
    xq = mxq(x, 2, "e4m3")
    h = x.transpose(1, 0, 2)[None]
    gi = (mxq(f64(agg), 3, "e4m3") @ unpack_weight(wih_words, wih_scales, "e4m3")) + f64(bih)
    gh = (xq.transpose(1, 0, 2)[None] @ unpack_weight(whh_words, whh_scales, "e4m3")) + f64(bhh)
    r = sigmoid(gi[..., :O] + gh[..., :O])
    z = sigmoid(gi[..., O:O + O] + gh[..., O:O + O])
    n = np.tanh(gi[..., O + O:] + r * gh[..., O + O:])
    hnew = (1.0 - z) * n + z * h
    upd = np.maximum(hnew.sum(0).transpose(1, 0, 2), 0.0)
    t = np.maximum((xq @ unpack_weight(wh_words, wh_scales, "e4m3")) + f64(bh), 0.0)
    return upd * t + x * (1.0 - t)

@@ -1,0 +1,270 @@
+from contextlib import ExitStack
+
+import concourse.mybir as mybir
+from concourse.masks import make_identity
+
+F32 = mybir.dt.float32
+BF16 = mybir.dt.bfloat16
+I32 = mybir.dt.int32
+U32 = mybir.dt.uint32
+U8 = mybir.dt.uint8
+FP8X4 = mybir.dt.float8_e4m3fn_x4
+ACT = mybir.ActivationFunctionType
+ALU = mybir.AluOpType
+
+P = 128
+DIRS = 3
+NODES = 1024
+FEAT = 512
+CHUNK = 512
+TILES = CHUNK // P
+CHUNKS = NODES // CHUNK
+BLOCKS = FEAT // P
+R_COL = 0
+Z_COL = FEAT
+N_COL = 2 * FEAT
+BIH_ROW = 0
+BHH_ROW = 3 * BLOCKS
+BH_ROW = 6 * BLOCKS
+
+FLOPS = 2 * FEAT * NODES * (DIRS * 3 * FEAT + 3 * FEAT + FEAT)
+
+
+def tile_graphconvolution_pb_kernel(
+    tc, agg, x, wih_words, wih_scales, whh_words, whh_scales, bih, bhh, wh_words, wh_scales, bh, out
+):
+    nc = tc.nc
+    with ExitStack() as ctx:
+        const = ctx.enter_context(tc.tile_pool(name="const", bufs=1))
+        stage = ctx.enter_context(tc.tile_pool(name="stage", bufs=3))
+        work = ctx.enter_context(tc.tile_pool(name="work", bufs=2))
+        psum = ctx.enter_context(tc.psum_pool(name="psum", bufs=1))
+
+        def load_scales(scales, label):
+            plane = const.tile([P, scales.shape[2]], U8, name=label + "_plane", align_bytes=64)
+            nc.vector.memset(plane[:].bitcast(I32), 0)
+            for quad in range(4):
+                nc.sync.dma_start(
+                    out=plane[32 * quad : 32 * quad + 4, :].bitcast(I32),
+                    in_=scales[0, 4 * quad : 4 * quad + 4, :].bitcast(I32),
+                )
+            return plane
+
+        def load_codes(words, label):
+            codes = const.tile([P, 4 * words.shape[2]], U8, name=label + "_codes", align_bytes=64)
+            nc.sync.dma_start(
+                out=codes[:].bitcast(I32), in_=words[0].rearrange("p n t -> p (n t)").bitcast(I32)
+            )
+            return codes
+
+        whh_plane = load_scales(whh_scales, "whh")
+        wih_plane = load_scales(wih_scales, "wih")
+        wh_plane = load_scales(wh_scales, "wh")
+        whh_w = (load_codes(whh_words, "whh"), whh_plane)
+        wih_w = (load_codes(wih_words, "wih"), wih_plane)
+        wh_w = (load_codes(wh_words, "wh"), wh_plane)
+
+        sources = [x[:, 0, :]] + [agg[d, 0] for d in range(DIRS)]
+        raw = {}
+        for c in range(CHUNKS):
+            for s, rows in enumerate(sources):
+                raw[s, c] = const.tile([P, TILES, FEAT], BF16, name="raw%d_%d" % (s, c))
+                nc.scalar.dma_start(
+                    out=raw[s, c][:],
+                    in_=rows.rearrange("(c p a) k -> c p a k", p=P, a=TILES)[c],
+                )
+        out_rows = out[:, 0, :].rearrange("(c p a) f -> c p a f", p=P, a=TILES)
+
+        ident_f32 = const.tile([P, P], F32)
+        make_identity(nc, ident_f32[:])
+        ident_bf = const.tile([P, P], BF16)
+        make_identity(nc, ident_bf[:])
+        three_ident = const.tile([P, P], BF16)
+        nc.vector.tensor_scalar(
+            out=three_ident[:], in0=ident_bf[:], scalar1=3.0, scalar2=None, op0=ALU.mult
+        )
+
+        warm = const.tile([P, 1], F32)
+        nc.vector.memset(warm[:], 0.0)
+        nc.scalar.activation(out=warm[:], in_=warm[:], func=ACT.Sigmoid)
+
+        bias_rows = const.tile([P, P], BF16)
+        nc.vector.memset(bias_rows[:], 0.0)
+        for first_row, vector in ((BIH_ROW, bih), (BHH_ROW, bhh), (BH_ROW, bh)):
+            as_rows = vector.rearrange("(r f) -> r f", f=P)
+            nc.gpsimd.dma_start(
+                out=bias_rows[first_row : first_row + as_rows.shape[0], :], in_=as_rows
+            )
+        bias_bank = psum.tile([P, P], BF16, tag="gate", bufs=3)
+        nc.tensor.transpose(bias_bank[:], bias_rows[:], ident_bf[:])
+        bias = const.tile([P, P], F32)
+        nc.vector.tensor_copy(out=bias[:], in_=bias_bank[:])
+        r_bias = const.tile([P, BLOCKS], F32)
+        nc.vector.tensor_tensor(
+            out=r_bias[:],
+            in0=bias[:, BIH_ROW : BIH_ROW + BLOCKS],
+            in1=bias[:, BHH_ROW : BHH_ROW + BLOCKS],
+            op=ALU.add,
+        )
+        neg_z_bias = const.tile([P, BLOCKS], F32)
+        nc.vector.scalar_tensor_tensor(
+            out=neg_z_bias[:],
+            in0=bias[:, BIH_ROW + BLOCKS : BIH_ROW + 2 * BLOCKS],
+            scalar=-1.0,
+            in1=bias[:, BHH_ROW + BLOCKS : BHH_ROW + 2 * BLOCKS],
+            op0=ALU.mult,
+            op1=ALU.subtract,
+        )
+
+        quantised = {}
+
+        def quantise(s, c):
+            pairs = raw[s, c][:].rearrange("p a k -> p (a k)").bitcast(F32)
+            grouped = stage.tile([P, 4 * CHUNK], BF16, align_bytes=64)
+            grouped_words = grouped[:].bitcast(F32).rearrange("p (m u) -> p m u", u=2)
+            for half in range(2):
+                bank = psum.tile([P, 2, 2 * P], F32, tag="gate", bufs=3)
+                for a in (2 * half, 2 * half + 1):
+                    first = a * FEAT // 2
+                    for u in range(2):
+                        nc.tensor.transpose(
+                            bank[:, u, (a % 2) * P : (a % 2 + 1) * P],
+                            pairs[:, first + u : first + FEAT // 2 : 2],
+                            ident_f32[:],
+                        )
+                nc.scalar.copy(
+                    out=grouped_words[:, 2 * P * half : 2 * P * (half + 1), :],
+                    in_=bank[:].rearrange("p u m -> p m u"),
+                )
+            codes = const.tile([P, CHUNK], U32, name="codes%d_%d" % (s, c), align_bytes=64)
+            plane = const.tile([P, CHUNK], U8, name="plane%d_%d" % (s, c), align_bytes=64)
+            nc.vector.quantize_mx(out=codes[:].bitcast(FP8X4), scales=plane[:], in_=grouped[:])
+            quantised[s, c] = (codes, plane)
+
+        x_by_feature = {}
+
+        def transpose_x(c):
+            x_by_feature[c] = const.tile([P, BLOCKS, CHUNK], BF16, name="xT%d" % c)
+            for half in range(2):
+                bank = psum.tile([P, 2, CHUNK], BF16, tag="gate", bufs=3)
+                for j in (2 * half, 2 * half + 1):
+                    for a in range(TILES):
+                        nc.tensor.transpose(
+                            bank[:, j % 2, a * P : (a + 1) * P],
+                            raw[0, c][:, a, j * P : (j + 1) * P],
+                            ident_bf[:],
+                        )
+                nc.scalar.copy(out=x_by_feature[c][:, 2 * half : 2 * half + 2, :], in_=bank[:])
+
+        def mx_pass(bank, weight, first_col, s, c, start, stop):
+            w_codes, w_plane = weight
+            a_codes, a_plane = quantised[s, c]
+            nc.tensor.matmul_mx(
+                out=bank[:],
+                lhsT=w_codes[:, 4 * first_col : 4 * (first_col + P)].bitcast(FP8X4),
+                lhsT_scale=w_plane[:, first_col : first_col + P],
+                rhs=a_codes[:].bitcast(FP8X4),
+                rhs_scale=a_plane[:],
+                start=start,
+                stop=stop,
+            )
+
+        def column(table, i):
+            return table[:, i : i + 1]
+
+        for s in range(1 + DIRS):
+            quantise(s, 0)
+        transpose_x(0)
+
+        for c in range(CHUNKS):
+            for j in range(BLOCKS):
+                feats = slice(j * P, (j + 1) * P)
+
+                if c + 1 < CHUNKS:
+                    quantise(j, c + 1)
+                    if j == 0:
+                        transpose_x(c + 1)
+
+                hn_bank = psum.tile([P, CHUNK], F32, tag="hn", bufs=1)
+                mx_pass(hn_bank, whh_w, N_COL + j * P, 0, c, True, True)
+                t_bank = psum.tile([P, CHUNK], F32, tag="gate", bufs=3)
+                mx_pass(t_bank, wh_w, j * P, 0, c, True, True)
+                t_gate = work.tile([P, CHUNK], F32)
+                nc.scalar.activation(
+                    out=t_gate[:], in_=t_bank[:], func=ACT.Relu, bias=column(bias, BH_ROW + j)
+                )
+
+                r_gate = work.tile([P, DIRS, CHUNK], F32)
+                keep = work.tile([P, DIRS, CHUNK], F32)
+                cand = work.tile([P, DIRS, CHUNK], F32)
+                for d in range(DIRS):
+                    r_bank = psum.tile([P, CHUNK], F32, tag="gate", bufs=3)
+                    mx_pass(r_bank, wih_w, R_COL + j * P, 1 + d, c, True, False)
+                    mx_pass(r_bank, whh_w, R_COL + j * P, 0, c, False, True)
+                    nc.scalar.activation(
+                        out=r_gate[:, d, :], in_=r_bank[:], func=ACT.Sigmoid, bias=column(r_bias, j)
+                    )
+                    z_bank = psum.tile([P, CHUNK], F32, tag="gate", bufs=3)
+                    mx_pass(z_bank, wih_w, Z_COL + j * P, 1 + d, c, True, False)
+                    mx_pass(z_bank, whh_w, Z_COL + j * P, 0, c, False, True)
+                    nc.scalar.activation(
+                        out=keep[:, d, :],
+                        in_=z_bank[:],
+                        func=ACT.Sigmoid,
+                        bias=column(neg_z_bias, j),
+                        scale=-1.0,
+                    )
+                    in_bank = psum.tile([P, CHUNK], F32, tag="in", bufs=2)
+                    mx_pass(in_bank, wih_w, N_COL + j * P, 1 + d, c, True, True)
+                    nc.vector.scalar_tensor_tensor(
+                        out=cand[:, d, :],
+                        in0=hn_bank[:],
+                        scalar=column(bias, BHH_ROW + 2 * BLOCKS + j),
+                        in1=r_gate[:, d, :],
+                        op0=ALU.add,
+                        op1=ALU.mult,
+                    )
+                    nc.vector.tensor_tensor(
+                        out=cand[:, d, :], in0=in_bank[:], in1=cand[:, d, :], op=ALU.add
+                    )
+                    nc.scalar.activation(
+                        out=cand[:, d, :],
+                        in_=cand[:, d, :],
+                        func=ACT.Tanh,
+                        bias=column(bias, BIH_ROW + 2 * BLOCKS + j),
+                    )
+
+                h_all = x_by_feature[c][:, j, :].unsqueeze(1).to_broadcast([P, DIRS, CHUNK])
+                nc.vector.tensor_tensor(out=cand[:], in0=cand[:], in1=h_all, op=ALU.subtract)
+                nc.vector.tensor_tensor(out=cand[:], in0=cand[:], in1=keep[:], op=ALU.mult)
+
+                sum_bank = psum.tile([P, TILES, P], F32, tag="back", bufs=2)
+                for a in range(TILES):
+                    nc.tensor.matmul(
+                        sum_bank[:, a, :],
+                        lhsT=three_ident[:],
+                        rhs=raw[0, c][:, a, feats],
+                        start=True,
+                        stop=False,
+                    )
+                    for d in range(DIRS):
+                        nc.tensor.matmul(
+                            sum_bank[:, a, :],
+                            lhsT=cand[:, d, a * P : (a + 1) * P],
+                            rhs=ident_f32[:],
+                            is_transpose=True,
+                            start=False,
+                            stop=(d == DIRS - 1),
+                        )
+                t_back = psum.tile([P, TILES, P], F32, tag="back", bufs=2)
+                for a in range(TILES):
+                    nc.tensor.transpose(t_back[:, a, :], t_gate[:, a * P : (a + 1) * P], ident_f32[:])
+
+                x_block = raw[0, c][:, :, feats]
+                result = work.tile([P, TILES, P], F32)
+                nc.vector.scalar_tensor_tensor(
+                    out=result[:], in0=sum_bank[:], scalar=0.0, in1=x_block, op0=ALU.max, op1=ALU.subtract
+                )
+                nc.vector.tensor_tensor(out=result[:], in0=result[:], in1=t_back[:], op=ALU.mult)
+                nc.vector.tensor_tensor(out=result[:], in0=result[:], in1=x_block, op=ALU.add)
+                nc.sync.dma_start(out=out_rows[c][:, :, feats], in_=result[:])

@@ -16,18 +16,21 @@ P = 128
 DIRS = 3
 NODES = 1024
 FEAT = 512
+GATES = 3
 CHUNK = 512
 TILES = CHUNK // P
 CHUNKS = NODES // CHUNK
 BLOCKS = FEAT // P
+STEPS = CHUNKS * BLOCKS * DIRS
 R_COL = 0
 Z_COL = FEAT
 N_COL = 2 * FEAT
 BIH_ROW = 0
-BHH_ROW = 3 * BLOCKS
-BH_ROW = 6 * BLOCKS
+BHH_ROW = GATES * BLOCKS
+BH_ROW = 2 * GATES * BLOCKS
+BACK_LAG = 2
 
-FLOPS = 2 * FEAT * NODES * (DIRS * 3 * FEAT + 3 * FEAT + FEAT)
+FLOPS = 2 * FEAT * NODES * (DIRS * GATES * FEAT + GATES * FEAT + FEAT)
 
 
 def tile_graphconvolution_pb_kernel(
@@ -35,10 +38,25 @@ def tile_graphconvolution_pb_kernel(
 ):
     nc = tc.nc
     with ExitStack() as ctx:
+        ctx.enter_context(tc.manual_schedule())
         const = ctx.enter_context(tc.tile_pool(name="const", bufs=1))
         stage = ctx.enter_context(tc.tile_pool(name="stage", bufs=3))
-        work = ctx.enter_context(tc.tile_pool(name="work", bufs=2))
+        work = ctx.enter_context(tc.tile_pool(name="work", bufs=3))
         psum = ctx.enter_context(tc.psum_pool(name="psum", bufs=1))
+
+        warm = const.tile([P, 1], F32)
+        nc.vector.memset(warm[:], 0.0)
+        nc.scalar.activation(out=warm[:], in_=warm[:], func=ACT.Sigmoid)
+
+        sources = [x[:, 0, :]] + [agg[d, 0] for d in range(DIRS)]
+        raw = {}
+
+        def load_source(s, c):
+            raw[s, c] = const.tile([P, TILES, FEAT], BF16, name="raw%d_%d" % (s, c))
+            nc.sync.dma_start(
+                out=raw[s, c][:],
+                in_=sources[s].rearrange("(c p a) k -> c p a k", p=P, a=TILES)[c],
+            )
 
         def load_scales(scales, label):
             plane = const.tile([P, scales.shape[2]], U8, name=label + "_plane", align_bytes=64)
@@ -50,29 +68,43 @@ def tile_graphconvolution_pb_kernel(
                 )
             return plane
 
-        def load_codes(words, label):
-            codes = const.tile([P, 4 * words.shape[2]], U8, name=label + "_codes", align_bytes=64)
+        def as_int32(words):
+            return words[0].rearrange("p n t -> p (n t)").bitcast(I32)
+
+        def load_gate_codes(codes, words, j):
+            by_block = "p (g j n) -> p g j n"
             nc.sync.dma_start(
-                out=codes[:].bitcast(I32), in_=words[0].rearrange("p n t -> p (n t)").bitcast(I32)
+                out=codes[:].bitcast(I32).rearrange(by_block, g=GATES, j=BLOCKS)[:, :, j, :],
+                in_=as_int32(words).rearrange(by_block, g=GATES, j=BLOCKS)[:, :, j, :],
             )
-            return codes
 
+        bias_rows = const.tile([P, P], BF16)
+        nc.vector.memset(bias_rows[:], 0.0)
+        for first_row, vector in ((BIH_ROW, bih), (BHH_ROW, bhh), (BH_ROW, bh)):
+            as_rows = vector.rearrange("(r f) -> r f", f=P)
+            nc.gpsimd.dma_start(
+                out=bias_rows[first_row : first_row + as_rows.shape[0], :], in_=as_rows
+            )
         whh_plane = load_scales(whh_scales, "whh")
+        for s in range(1 + DIRS):
+            load_source(s, 0)
         wih_plane = load_scales(wih_scales, "wih")
+        whh_codes = const.tile([P, 4 * GATES * FEAT], U8, align_bytes=64)
+        wih_codes = const.tile([P, 4 * GATES * FEAT], U8, align_bytes=64)
+        wh_codes = const.tile([P, 4 * FEAT], U8, align_bytes=64)
+        load_gate_codes(whh_codes, whh_words, 0)
+        load_gate_codes(wih_codes, wih_words, 0)
         wh_plane = load_scales(wh_scales, "wh")
-        whh_w = (load_codes(whh_words, "whh"), whh_plane)
-        wih_w = (load_codes(wih_words, "wih"), wih_plane)
-        wh_w = (load_codes(wh_words, "wh"), wh_plane)
-
-        sources = [x[:, 0, :]] + [agg[d, 0] for d in range(DIRS)]
-        raw = {}
-        for c in range(CHUNKS):
-            for s, rows in enumerate(sources):
-                raw[s, c] = const.tile([P, TILES, FEAT], BF16, name="raw%d_%d" % (s, c))
-                nc.scalar.dma_start(
-                    out=raw[s, c][:],
-                    in_=rows.rearrange("(c p a) k -> c p a k", p=P, a=TILES)[c],
-                )
+        nc.sync.dma_start(out=wh_codes[:].bitcast(I32), in_=as_int32(wh_words))
+        for j in range(1, BLOCKS):
+            load_gate_codes(whh_codes, whh_words, j)
+            load_gate_codes(wih_codes, wih_words, j)
+        for c in range(1, CHUNKS):
+            for s in range(1 + DIRS):
+                load_source(s, c)
+        whh_w = (whh_codes, whh_plane)
+        wih_w = (wih_codes, wih_plane)
+        wh_w = (wh_codes, wh_plane)
         out_rows = out[:, 0, :].rearrange("(c p a) f -> c p a f", p=P, a=TILES)
 
         ident_f32 = const.tile([P, P], F32)
@@ -84,44 +116,40 @@ def tile_graphconvolution_pb_kernel(
             out=three_ident[:], in0=ident_bf[:], scalar1=3.0, scalar2=None, op0=ALU.mult
         )
 
-        warm = const.tile([P, 1], F32)
-        nc.vector.memset(warm[:], 0.0)
-        nc.scalar.activation(out=warm[:], in_=warm[:], func=ACT.Sigmoid)
-
-        bias_rows = const.tile([P, P], BF16)
-        nc.vector.memset(bias_rows[:], 0.0)
-        for first_row, vector in ((BIH_ROW, bih), (BHH_ROW, bhh), (BH_ROW, bh)):
-            as_rows = vector.rearrange("(r f) -> r f", f=P)
-            nc.gpsimd.dma_start(
-                out=bias_rows[first_row : first_row + as_rows.shape[0], :], in_=as_rows
-            )
-        bias_bank = psum.tile([P, P], BF16, tag="gate", bufs=3)
-        nc.tensor.transpose(bias_bank[:], bias_rows[:], ident_bf[:])
         bias = const.tile([P, P], F32)
-        nc.vector.tensor_copy(out=bias[:], in_=bias_bank[:])
         r_bias = const.tile([P, BLOCKS], F32)
-        nc.vector.tensor_tensor(
-            out=r_bias[:],
-            in0=bias[:, BIH_ROW : BIH_ROW + BLOCKS],
-            in1=bias[:, BHH_ROW : BHH_ROW + BLOCKS],
-            op=ALU.add,
-        )
         neg_z_bias = const.tile([P, BLOCKS], F32)
-        nc.vector.scalar_tensor_tensor(
-            out=neg_z_bias[:],
-            in0=bias[:, BIH_ROW + BLOCKS : BIH_ROW + 2 * BLOCKS],
-            scalar=-1.0,
-            in1=bias[:, BHH_ROW + BLOCKS : BHH_ROW + 2 * BLOCKS],
-            op0=ALU.mult,
-            op1=ALU.subtract,
-        )
 
+        def spread_biases():
+            bias_bank = psum.tile([P, P], BF16, tag="gate", bufs=3)
+            nc.tensor.transpose(bias_bank[:], bias_rows[:], ident_bf[:])
+            nc.vector.tensor_copy(out=bias[:], in_=bias_bank[:])
+            nc.vector.tensor_tensor(
+                out=r_bias[:],
+                in0=bias[:, BIH_ROW : BIH_ROW + BLOCKS],
+                in1=bias[:, BHH_ROW : BHH_ROW + BLOCKS],
+                op=ALU.add,
+            )
+            nc.vector.scalar_tensor_tensor(
+                out=neg_z_bias[:],
+                in0=bias[:, BIH_ROW + BLOCKS : BIH_ROW + 2 * BLOCKS],
+                scalar=-1.0,
+                in1=bias[:, BHH_ROW + BLOCKS : BHH_ROW + 2 * BLOCKS],
+                op0=ALU.mult,
+                op1=ALU.subtract,
+            )
+
+        def column(table, i):
+            return table[:, i : i + 1]
+
+        grouped = {}
         quantised = {}
+        x_by_feature = {}
 
-        def quantise(s, c):
+        def transpose_source(s, c):
             pairs = raw[s, c][:].rearrange("p a k -> p (a k)").bitcast(F32)
-            grouped = stage.tile([P, 4 * CHUNK], BF16, align_bytes=64)
-            grouped_words = grouped[:].bitcast(F32).rearrange("p (m u) -> p m u", u=2)
+            grouped[s, c] = stage.tile([P, 4 * CHUNK], BF16, name="grouped", align_bytes=64)
+            grouped_pairs = grouped[s, c][:].bitcast(F32).rearrange("p (m u) -> p m u", u=2)
             for half in range(2):
                 bank = psum.tile([P, 2, 2 * P], F32, tag="gate", bufs=3)
                 for a in (2 * half, 2 * half + 1):
@@ -133,15 +161,9 @@ def tile_graphconvolution_pb_kernel(
                             ident_f32[:],
                         )
                 nc.scalar.copy(
-                    out=grouped_words[:, 2 * P * half : 2 * P * (half + 1), :],
+                    out=grouped_pairs[:, 2 * P * half : 2 * P * (half + 1), :],
                     in_=bank[:].rearrange("p u m -> p m u"),
                 )
-            codes = const.tile([P, CHUNK], U32, name="codes%d_%d" % (s, c), align_bytes=64)
-            plane = const.tile([P, CHUNK], U8, name="plane%d_%d" % (s, c), align_bytes=64)
-            nc.vector.quantize_mx(out=codes[:].bitcast(FP8X4), scales=plane[:], in_=grouped[:])
-            quantised[s, c] = (codes, plane)
-
-        x_by_feature = {}
 
         def transpose_x(c):
             x_by_feature[c] = const.tile([P, BLOCKS, CHUNK], BF16, name="xT%d" % c)
@@ -156,6 +178,14 @@ def tile_graphconvolution_pb_kernel(
                         )
                 nc.scalar.copy(out=x_by_feature[c][:, 2 * half : 2 * half + 2, :], in_=bank[:])
 
+        def quantise_source(s, c):
+            codes = const.tile([P, CHUNK], U32, name="codes%d_%d" % (s, c), align_bytes=64)
+            plane = const.tile([P, CHUNK], U8, name="plane%d_%d" % (s, c), align_bytes=64)
+            nc.vector.quantize_mx(
+                out=codes[:].bitcast(FP8X4), scales=plane[:], in_=grouped[s, c][:]
+            )
+            quantised[s, c] = (codes, plane)
+
         def mx_pass(bank, weight, first_col, s, c, start, stop):
             w_codes, w_plane = weight
             a_codes, a_plane = quantised[s, c]
@@ -169,102 +199,133 @@ def tile_graphconvolution_pb_kernel(
                 stop=stop,
             )
 
-        def column(table, i):
-            return table[:, i : i + 1]
+        unit_tiles = {}
+        step_tiles = {}
 
-        for s in range(1 + DIRS):
-            quantise(s, 0)
-        transpose_x(0)
-
-        for c in range(CHUNKS):
-            for j in range(BLOCKS):
-                feats = slice(j * P, (j + 1) * P)
-
-                if c + 1 < CHUNKS:
-                    quantise(j, c + 1)
-                    if j == 0:
-                        transpose_x(c + 1)
-
-                hn_bank = psum.tile([P, CHUNK], F32, tag="hn", bufs=1)
+        def gates(step):
+            unit, d = divmod(step, DIRS)
+            c, j = divmod(unit, BLOCKS)
+            if d == 0:
+                unit_tiles[unit] = (
+                    psum.tile([P, CHUNK], F32, name="hn_bank", tag="hn", bufs=1),
+                    work.tile([P, CHUNK], F32, name="t_gate"),
+                )
+            hn_bank, t_gate = unit_tiles[unit]
+            step_tiles[step] = (
+                psum.tile([P, CHUNK], F32, name="in_bank", tag="in", bufs=2),
+                work.tile([P, CHUNK], F32, name="r_gate"),
+                work.tile([P, CHUNK], F32, name="keep"),
+                work.tile([P, CHUNK], F32, name="cand", bufs=DIRS + 2 + BACK_LAG),
+            )
+            in_bank, r_gate, keep, cand = step_tiles[step]
+            r_bank = psum.tile([P, CHUNK], F32, tag="gate", bufs=3)
+            mx_pass(r_bank, wih_w, R_COL + j * P, 1 + d, c, True, False)
+            mx_pass(r_bank, whh_w, R_COL + j * P, 0, c, False, True)
+            nc.scalar.activation(
+                out=r_gate[:], in_=r_bank[:], func=ACT.Sigmoid, bias=column(r_bias, j)
+            )
+            z_bank = psum.tile([P, CHUNK], F32, tag="gate", bufs=3)
+            mx_pass(z_bank, wih_w, Z_COL + j * P, 1 + d, c, True, False)
+            mx_pass(z_bank, whh_w, Z_COL + j * P, 0, c, False, True)
+            nc.scalar.activation(
+                out=keep[:],
+                in_=z_bank[:],
+                func=ACT.Sigmoid,
+                bias=column(neg_z_bias, j),
+                scale=-1.0,
+            )
+            if d == 0:
                 mx_pass(hn_bank, whh_w, N_COL + j * P, 0, c, True, True)
+            mx_pass(in_bank, wih_w, N_COL + j * P, 1 + d, c, True, True)
+            if d == 0:
                 t_bank = psum.tile([P, CHUNK], F32, tag="gate", bufs=3)
                 mx_pass(t_bank, wh_w, j * P, 0, c, True, True)
-                t_gate = work.tile([P, CHUNK], F32)
                 nc.scalar.activation(
                     out=t_gate[:], in_=t_bank[:], func=ACT.Relu, bias=column(bias, BH_ROW + j)
                 )
 
-                r_gate = work.tile([P, DIRS, CHUNK], F32)
-                keep = work.tile([P, DIRS, CHUNK], F32)
-                cand = work.tile([P, DIRS, CHUNK], F32)
-                for d in range(DIRS):
-                    r_bank = psum.tile([P, CHUNK], F32, tag="gate", bufs=3)
-                    mx_pass(r_bank, wih_w, R_COL + j * P, 1 + d, c, True, False)
-                    mx_pass(r_bank, whh_w, R_COL + j * P, 0, c, False, True)
-                    nc.scalar.activation(
-                        out=r_gate[:, d, :], in_=r_bank[:], func=ACT.Sigmoid, bias=column(r_bias, j)
-                    )
-                    z_bank = psum.tile([P, CHUNK], F32, tag="gate", bufs=3)
-                    mx_pass(z_bank, wih_w, Z_COL + j * P, 1 + d, c, True, False)
-                    mx_pass(z_bank, whh_w, Z_COL + j * P, 0, c, False, True)
-                    nc.scalar.activation(
-                        out=keep[:, d, :],
-                        in_=z_bank[:],
-                        func=ACT.Sigmoid,
-                        bias=column(neg_z_bias, j),
-                        scale=-1.0,
-                    )
-                    in_bank = psum.tile([P, CHUNK], F32, tag="in", bufs=2)
-                    mx_pass(in_bank, wih_w, N_COL + j * P, 1 + d, c, True, True)
-                    nc.vector.scalar_tensor_tensor(
-                        out=cand[:, d, :],
-                        in0=hn_bank[:],
-                        scalar=column(bias, BHH_ROW + 2 * BLOCKS + j),
-                        in1=r_gate[:, d, :],
-                        op0=ALU.add,
-                        op1=ALU.mult,
-                    )
-                    nc.vector.tensor_tensor(
-                        out=cand[:, d, :], in0=in_bank[:], in1=cand[:, d, :], op=ALU.add
-                    )
-                    nc.scalar.activation(
-                        out=cand[:, d, :],
-                        in_=cand[:, d, :],
-                        func=ACT.Tanh,
-                        bias=column(bias, BIH_ROW + 2 * BLOCKS + j),
-                    )
+        def candidate(step):
+            unit = step // DIRS
+            j = unit % BLOCKS
+            hn_bank, t_gate = unit_tiles[unit]
+            in_bank, r_gate, keep, cand = step_tiles[step]
+            nc.vector.scalar_tensor_tensor(
+                out=cand[:],
+                in0=hn_bank[:],
+                scalar=column(bias, BHH_ROW + 2 * BLOCKS + j),
+                in1=r_gate[:],
+                op0=ALU.add,
+                op1=ALU.mult,
+            )
+            nc.vector.tensor_tensor(out=cand[:], in0=in_bank[:], in1=cand[:], op=ALU.add)
 
-                h_all = x_by_feature[c][:, j, :].unsqueeze(1).to_broadcast([P, DIRS, CHUNK])
-                nc.vector.tensor_tensor(out=cand[:], in0=cand[:], in1=h_all, op=ALU.subtract)
-                nc.vector.tensor_tensor(out=cand[:], in0=cand[:], in1=keep[:], op=ALU.mult)
+        def blend(step):
+            c, j = divmod(step // DIRS, BLOCKS)
+            in_bank, r_gate, keep, cand = step_tiles[step]
+            nc.scalar.activation(
+                out=cand[:], in_=cand[:], func=ACT.Tanh, bias=column(bias, BIH_ROW + 2 * BLOCKS + j)
+            )
+            nc.vector.tensor_tensor(
+                out=cand[:], in0=cand[:], in1=x_by_feature[c][:, j, :], op=ALU.subtract
+            )
+            nc.gpsimd.tensor_tensor(out=cand[:], in0=cand[:], in1=keep[:], op=ALU.mult)
 
-                sum_bank = psum.tile([P, TILES, P], F32, tag="back", bufs=2)
+        def finish(unit):
+            c, j = divmod(unit, BLOCKS)
+            feats = slice(j * P, (j + 1) * P)
+            hn_bank, t_gate = unit_tiles[unit]
+            x_block = raw[0, c][:, :, feats]
+            t_back = psum.tile([P, TILES, P], F32, tag="back", bufs=2)
+            for a in range(TILES):
+                nc.tensor.transpose(t_back[:, a, :], t_gate[:, a * P : (a + 1) * P], ident_f32[:])
+            sum_bank = psum.tile([P, TILES, P], F32, tag="back", bufs=2)
+            nc.tensor.matmul(sum_bank[:], lhsT=three_ident[:], rhs=x_block, start=True, stop=False)
+            for d in range(DIRS):
+                in_bank, r_gate, keep, cand = step_tiles[unit * DIRS + d]
                 for a in range(TILES):
                     nc.tensor.matmul(
                         sum_bank[:, a, :],
-                        lhsT=three_ident[:],
-                        rhs=raw[0, c][:, a, feats],
-                        start=True,
-                        stop=False,
+                        lhsT=cand[:, a * P : (a + 1) * P],
+                        rhs=ident_f32[:],
+                        is_transpose=True,
+                        start=False,
+                        stop=(d == DIRS - 1 and a == TILES - 1),
                     )
-                    for d in range(DIRS):
-                        nc.tensor.matmul(
-                            sum_bank[:, a, :],
-                            lhsT=cand[:, d, a * P : (a + 1) * P],
-                            rhs=ident_f32[:],
-                            is_transpose=True,
-                            start=False,
-                            stop=(d == DIRS - 1),
-                        )
-                t_back = psum.tile([P, TILES, P], F32, tag="back", bufs=2)
-                for a in range(TILES):
-                    nc.tensor.transpose(t_back[:, a, :], t_gate[:, a * P : (a + 1) * P], ident_f32[:])
+            result = work.tile([P, TILES, P], F32)
+            nc.vector.scalar_tensor_tensor(
+                out=result[:], in0=sum_bank[:], scalar=0.0, in1=x_block, op0=ALU.max, op1=ALU.subtract
+            )
+            nc.vector.tensor_tensor(out=result[:], in0=result[:], in1=t_back[:], op=ALU.mult)
+            nc.gpsimd.tensor_tensor(out=result[:], in0=result[:], in1=x_block, op=ALU.add)
+            nc.sync.dma_start(out=out_rows[c][:, :, feats], in_=result[:])
 
-                x_block = raw[0, c][:, :, feats]
-                result = work.tile([P, TILES, P], F32)
-                nc.vector.scalar_tensor_tensor(
-                    out=result[:], in0=sum_bank[:], scalar=0.0, in1=x_block, op0=ALU.max, op1=ALU.subtract
-                )
-                nc.vector.tensor_tensor(out=result[:], in0=result[:], in1=t_back[:], op=ALU.mult)
-                nc.vector.tensor_tensor(out=result[:], in0=result[:], in1=x_block, op=ALU.add)
-                nc.sync.dma_start(out=out_rows[c][:, :, feats], in_=result[:])
+        for s in range(1 + DIRS):
+            transpose_source(s, 0)
+            if s > 0:
+                quantise_source(s - 1, 0)
+            if s == 1:
+                spread_biases()
+        quantise_source(DIRS, 0)
+
+        transposed = []
+        for tick in range(STEPS + 1 + BACK_LAG):
+            if tick < STEPS:
+                gates(tick)
+                candidate(tick)
+            if 0 <= tick - 1 < STEPS:
+                blend(tick - 1)
+            ended = tick - 1 - BACK_LAG
+            if ended >= 0 and ended % DIRS == DIRS - 1:
+                finish(ended // DIRS)
+            for s, c in transposed:
+                quantise_source(s, c)
+            transposed = []
+            if tick == 0:
+                transpose_x(0)
+            unit, d = divmod(tick, DIRS)
+            c, j = divmod(unit, BLOCKS)
+            if c + 1 < CHUNKS and d == DIRS - 1:
+                transpose_source(j, c + 1)
+                transposed = [(j, c + 1)]
+                if j == 0:
+                    transpose_x(c + 1)

@@ -78,16 +78,11 @@ def tile_graphconvolution_pb_kernel(
                 in_=as_int32(words).rearrange(by_block, g=GATES, j=BLOCKS)[:, :, j, :],
             )
 
-        bias_rows = const.tile([P, P], BF16)
-        nc.vector.memset(bias_rows[:], 0.0)
-        for first_row, vector in ((BIH_ROW, bih), (BHH_ROW, bhh), (BH_ROW, bh)):
-            as_rows = vector.rearrange("(r f) -> r f", f=P)
-            nc.gpsimd.dma_start(
-                out=bias_rows[first_row : first_row + as_rows.shape[0], :], in_=as_rows
-            )
+        load_source(0, 0)
+        load_source(1, 0)
         whh_plane = load_scales(whh_scales, "whh")
-        for s in range(1 + DIRS):
-            load_source(s, 0)
+        load_source(2, 0)
+        load_source(3, 0)
         wih_plane = load_scales(wih_scales, "wih")
         whh_codes = const.tile([P, 4 * GATES * FEAT], U8, align_bytes=64)
         wih_codes = const.tile([P, 4 * GATES * FEAT], U8, align_bytes=64)
@@ -109,6 +104,13 @@ def tile_graphconvolution_pb_kernel(
 
         ident_f32 = const.tile([P, P], F32)
         make_identity(nc, ident_f32[:])
+        bias_rows = const.tile([P, P], BF16)
+        nc.vector.memset(bias_rows[:], 0.0)
+        for first_row, vector in ((BIH_ROW, bih), (BHH_ROW, bhh), (BH_ROW, bh)):
+            as_rows = vector.rearrange("(r f) -> r f", f=P)
+            nc.gpsimd.dma_start(
+                out=bias_rows[first_row : first_row + as_rows.shape[0], :], in_=as_rows
+            )
         ident_bf = const.tile([P, P], BF16)
         make_identity(nc, ident_bf[:])
         three_ident = const.tile([P, P], BF16)
@@ -214,7 +216,7 @@ def tile_graphconvolution_pb_kernel(
             step_tiles[step] = (
                 psum.tile([P, CHUNK], F32, name="in_bank", tag="in", bufs=2),
                 work.tile([P, CHUNK], F32, name="r_gate"),
-                work.tile([P, CHUNK], F32, name="keep"),
+                work.tile([P, CHUNK], F32, name="keep", bufs=4),
                 work.tile([P, CHUNK], F32, name="cand", bufs=DIRS + 2 + BACK_LAG),
             )
             in_bank, r_gate, keep, cand = step_tiles[step]
@@ -260,12 +262,14 @@ def tile_graphconvolution_pb_kernel(
             nc.vector.tensor_tensor(out=cand[:], in0=in_bank[:], in1=cand[:], op=ALU.add)
 
         def blend(step):
-            c, j = divmod(step // DIRS, BLOCKS)
+            unit, d = divmod(step, DIRS)
+            c, j = divmod(unit, BLOCKS)
             in_bank, r_gate, keep, cand = step_tiles[step]
             nc.scalar.activation(
                 out=cand[:], in_=cand[:], func=ACT.Tanh, bias=column(bias, BIH_ROW + 2 * BLOCKS + j)
             )
-            nc.vector.tensor_tensor(
+            subtract_engine = nc.gpsimd if d == 0 else nc.vector
+            subtract_engine.tensor_tensor(
                 out=cand[:], in0=cand[:], in1=x_by_feature[c][:, j, :], op=ALU.subtract
             )
             nc.gpsimd.tensor_tensor(out=cand[:], in0=cand[:], in1=keep[:], op=ALU.mult)

@@ -246,6 +246,9 @@ def tile_graphconvolution_pb_kernel(
                     out=t_gate[:], in_=t_bank[:], func=ACT.Relu, bias=column(bias, BH_ROW + j)
                 )
 
+        def helper(at_the_end):
+            return nc.vector if at_the_end else nc.gpsimd
+
         def candidate(step):
             unit = step // DIRS
             j = unit % BLOCKS
@@ -262,17 +265,17 @@ def tile_graphconvolution_pb_kernel(
             nc.vector.tensor_tensor(out=cand[:], in0=in_bank[:], in1=cand[:], op=ALU.add)
 
         def blend(step):
-            unit, d = divmod(step, DIRS)
-            c, j = divmod(unit, BLOCKS)
+            c, j = divmod(step // DIRS, BLOCKS)
             in_bank, r_gate, keep, cand = step_tiles[step]
             nc.scalar.activation(
                 out=cand[:], in_=cand[:], func=ACT.Tanh, bias=column(bias, BIH_ROW + 2 * BLOCKS + j)
             )
-            subtract_engine = nc.gpsimd if d == 0 else nc.vector
-            subtract_engine.tensor_tensor(
+            nc.vector.tensor_tensor(
                 out=cand[:], in0=cand[:], in1=x_by_feature[c][:, j, :], op=ALU.subtract
             )
-            nc.gpsimd.tensor_tensor(out=cand[:], in0=cand[:], in1=keep[:], op=ALU.mult)
+            helper(step == STEPS - 1).tensor_tensor(
+                out=cand[:], in0=cand[:], in1=keep[:], op=ALU.mult
+            )
 
         def finish(unit):
             c, j = divmod(unit, BLOCKS)
@@ -300,7 +303,9 @@ def tile_graphconvolution_pb_kernel(
                 out=result[:], in0=sum_bank[:], scalar=0.0, in1=x_block, op0=ALU.max, op1=ALU.subtract
             )
             nc.vector.tensor_tensor(out=result[:], in0=result[:], in1=t_back[:], op=ALU.mult)
-            nc.gpsimd.tensor_tensor(out=result[:], in0=result[:], in1=x_block, op=ALU.add)
+            helper(unit == STEPS // DIRS - 1).tensor_tensor(
+                out=result[:], in0=result[:], in1=x_block, op=ALU.add
+            )
             nc.sync.dma_start(out=out_rows[c][:, :, feats], in_=result[:])
 
         for s in range(1 + DIRS):

@@ -277,15 +277,23 @@ def tile_graphconvolution_pb_kernel(
                 out=cand[:], in0=cand[:], in1=keep[:], op=ALU.mult
             )
 
-        def finish(unit):
+        back_tiles = {}
+
+        def halves(unit):
+            if unit == STEPS // DIRS - 1:
+                return (slice(0, TILES // 2), slice(TILES // 2, TILES))
+            return (slice(0, TILES),)
+
+        def finish_back(unit):
             c, j = divmod(unit, BLOCKS)
-            feats = slice(j * P, (j + 1) * P)
             hn_bank, t_gate = unit_tiles[unit]
-            x_block = raw[0, c][:, :, feats]
-            t_back = psum.tile([P, TILES, P], F32, tag="back", bufs=2)
+            x_block = raw[0, c][:, :, j * P : (j + 1) * P]
+            last = unit == STEPS // DIRS - 1
+            tag, bufs = ("gate", 3) if last else ("back", 2)
+            t_back = psum.tile([P, TILES, P], F32, name="t_back", tag=tag, bufs=bufs)
             for a in range(TILES):
                 nc.tensor.transpose(t_back[:, a, :], t_gate[:, a * P : (a + 1) * P], ident_f32[:])
-            sum_bank = psum.tile([P, TILES, P], F32, tag="back", bufs=2)
+            sum_bank = psum.tile([P, TILES, P], F32, name="sum_bank", tag=tag, bufs=bufs)
             nc.tensor.matmul(sum_bank[:], lhsT=three_ident[:], rhs=x_block, start=True, stop=False)
             for d in range(DIRS):
                 in_bank, r_gate, keep, cand = step_tiles[unit * DIRS + d]
@@ -298,15 +306,36 @@ def tile_graphconvolution_pb_kernel(
                         start=False,
                         stop=(d == DIRS - 1 and a == TILES - 1),
                     )
-            result = work.tile([P, TILES, P], F32)
-            nc.vector.scalar_tensor_tensor(
-                out=result[:], in0=sum_bank[:], scalar=0.0, in1=x_block, op0=ALU.max, op1=ALU.subtract
-            )
-            nc.vector.tensor_tensor(out=result[:], in0=result[:], in1=t_back[:], op=ALU.mult)
-            helper(unit == STEPS // DIRS - 1).tensor_tensor(
-                out=result[:], in0=result[:], in1=x_block, op=ALU.add
-            )
-            nc.sync.dma_start(out=out_rows[c][:, :, feats], in_=result[:])
+            back_tiles[unit] = (t_back, sum_bank, work.tile([P, TILES, P], F32, name="result"))
+
+        def finish_relu(unit):
+            c, j = divmod(unit, BLOCKS)
+            x_block = raw[0, c][:, :, j * P : (j + 1) * P]
+            t_back, sum_bank, result = back_tiles[unit]
+            for part in halves(unit):
+                nc.vector.scalar_tensor_tensor(
+                    out=result[:, part, :],
+                    in0=sum_bank[:, part, :],
+                    scalar=0.0,
+                    in1=x_block[:, part, :],
+                    op0=ALU.max,
+                    op1=ALU.subtract,
+                )
+
+        def finish_rest(unit):
+            c, j = divmod(unit, BLOCKS)
+            feats = slice(j * P, (j + 1) * P)
+            x_block = raw[0, c][:, :, feats]
+            t_back, sum_bank, result = back_tiles[unit]
+            for part in halves(unit):
+                nc.vector.tensor_tensor(
+                    out=result[:, part, :], in0=result[:, part, :], in1=t_back[:, part, :], op=ALU.mult
+                )
+            for part in halves(unit):
+                helper(unit == STEPS // DIRS - 1).tensor_tensor(
+                    out=result[:, part, :], in0=result[:, part, :], in1=x_block[:, part, :], op=ALU.add
+                )
+                nc.sync.dma_start(out=out_rows[c][:, part, feats], in_=result[:, part, :])
 
         for s in range(1 + DIRS):
             transpose_source(s, 0)
@@ -323,9 +352,14 @@ def tile_graphconvolution_pb_kernel(
                 candidate(tick)
             if 0 <= tick - 1 < STEPS:
                 blend(tick - 1)
+            if tick == STEPS:
+                finish_rest(STEPS // DIRS - 2)
             ended = tick - 1 - BACK_LAG
             if ended >= 0 and ended % DIRS == DIRS - 1:
-                finish(ended // DIRS)
+                finish_back(ended // DIRS)
+                finish_relu(ended // DIRS)
+                if tick != STEPS - 1:
+                    finish_rest(ended // DIRS)
             for s, c in transposed:
                 quantise_source(s, c)
             transposed = []

@@ -167,18 +167,16 @@ def tile_graphconvolution_pb_kernel(
                     in_=bank[:].rearrange("p u m -> p m u"),
                 )
 
-        def transpose_x(c):
-            x_by_feature[c] = const.tile([P, BLOCKS, CHUNK], BF16, name="xT%d" % c)
-            for half in range(2):
-                bank = psum.tile([P, 2, CHUNK], BF16, tag="gate", bufs=3)
-                for j in (2 * half, 2 * half + 1):
-                    for a in range(TILES):
-                        nc.tensor.transpose(
-                            bank[:, j % 2, a * P : (a + 1) * P],
-                            raw[0, c][:, a, j * P : (j + 1) * P],
-                            ident_bf[:],
-                        )
-                nc.scalar.copy(out=x_by_feature[c][:, 2 * half : 2 * half + 2, :], in_=bank[:])
+        def transpose_x(unit):
+            c, j = divmod(unit, BLOCKS)
+            if j == 0:
+                x_by_feature[c] = const.tile([P, BLOCKS, CHUNK], BF16, name="xT%d" % c)
+            bank = psum.tile([P, CHUNK], BF16, tag="gate", bufs=3)
+            for a in range(TILES):
+                nc.tensor.transpose(
+                    bank[:, a * P : (a + 1) * P], raw[0, c][:, a, j * P : (j + 1) * P], ident_bf[:]
+                )
+            nc.scalar.copy(out=x_by_feature[c][:, j, :], in_=bank[:])
 
         def quantise_source(s, c):
             codes = const.tile([P, CHUNK], U32, name="codes%d_%d" % (s, c), align_bytes=64)
@@ -367,8 +365,8 @@ def tile_graphconvolution_pb_kernel(
                 transpose_x(0)
             unit, d = divmod(tick, DIRS)
             c, j = divmod(unit, BLOCKS)
+            if d == DIRS - 1 and unit + 1 < STEPS // DIRS:
+                transpose_x(unit + 1)
             if c + 1 < CHUNKS and d == DIRS - 1:
                 transpose_source(j, c + 1)
                 transposed = [(j, c + 1)]
-                if j == 0:
-                    transpose_x(c + 1)

@@ -339,7 +339,7 @@ def tile_graphconvolution_pb_kernel(
             transpose_source(s, 0)
             if s > 0:
                 quantise_source(s - 1, 0)
-            if s == 1:
+            if s == DIRS:
                 spread_biases()
         quantise_source(DIRS, 0)
 

@@ -237,7 +237,7 @@ def tile_graphconvolution_pb_kernel(
             if d == 0:
                 mx_pass(hn_bank, whh_w, N_COL + j * P, 0, c, True, True)
             mx_pass(in_bank, wih_w, N_COL + j * P, 1 + d, c, True, True)
-            if d == 0:
+            if d == 1:
                 t_bank = psum.tile([P, CHUNK], F32, tag="gate", bufs=3)
                 mx_pass(t_bank, wh_w, j * P, 0, c, True, True)
                 nc.scalar.activation(
@@ -252,15 +252,20 @@ def tile_graphconvolution_pb_kernel(
             j = unit % BLOCKS
             hn_bank, t_gate = unit_tiles[unit]
             in_bank, r_gate, keep, cand = step_tiles[step]
-            nc.vector.scalar_tensor_tensor(
-                out=cand[:],
-                in0=hn_bank[:],
-                scalar=column(bias, BHH_ROW + 2 * BLOCKS + j),
-                in1=r_gate[:],
-                op0=ALU.add,
-                op1=ALU.mult,
-            )
-            nc.vector.tensor_tensor(out=cand[:], in0=in_bank[:], in1=cand[:], op=ALU.add)
+            parts = (slice(0, CHUNK // 2), slice(CHUNK // 2, CHUNK))
+            for part in parts:
+                nc.vector.scalar_tensor_tensor(
+                    out=cand[:, part],
+                    in0=hn_bank[:, part],
+                    scalar=column(bias, BHH_ROW + 2 * BLOCKS + j),
+                    in1=r_gate[:, part],
+                    op0=ALU.add,
+                    op1=ALU.mult,
+                )
+            for part in parts:
+                nc.vector.tensor_tensor(
+                    out=cand[:, part], in0=in_bank[:, part], in1=cand[:, part], op=ALU.add
+                )
 
         def blend(step):
             c, j = divmod(step // DIRS, BLOCKS)
@@ -277,10 +282,10 @@ def tile_graphconvolution_pb_kernel(
 
         back_tiles = {}
 
+        HALVES = (slice(0, TILES // 2), slice(TILES // 2, TILES))
+
         def halves(unit):
-            if unit == STEPS // DIRS - 1:
-                return (slice(0, TILES // 2), slice(TILES // 2, TILES))
-            return (slice(0, TILES),)
+            return HALVES
 
         def finish_back(unit):
             c, j = divmod(unit, BLOCKS)
@@ -329,7 +334,7 @@ def tile_graphconvolution_pb_kernel(
                 nc.vector.tensor_tensor(
                     out=result[:, part, :], in0=result[:, part, :], in1=t_back[:, part, :], op=ALU.mult
                 )
-            for part in halves(unit):
+            for part in HALVES if unit == STEPS // DIRS - 1 else (slice(0, TILES),):
                 helper(unit == STEPS // DIRS - 1).tensor_tensor(
                     out=result[:, part, :], in0=result[:, part, :], in1=x_block[:, part, :], op=ALU.add
                 )
@@ -345,6 +350,9 @@ def tile_graphconvolution_pb_kernel(
 
         transposed = []
         for tick in range(STEPS + 1 + BACK_LAG):
+            for s, c in transposed:
+                quantise_source(s, c)
+            transposed = []
             if tick < STEPS:
                 gates(tick)
                 candidate(tick)
@@ -358,9 +366,6 @@ def tile_graphconvolution_pb_kernel(
                 finish_relu(ended // DIRS)
                 if tick != STEPS - 1:
                     finish_rest(ended // DIRS)
-            for s, c in transposed:
-                quantise_source(s, c)
-            transposed = []
             if tick == 0:
                 transpose_x(0)
             unit, d = divmod(tick, DIRS)

@@ -199,8 +199,21 @@ def tile_graphconvolution_pb_kernel(
                 stop=stop,
             )
 
+        PARTS = (slice(0, CHUNK // 2), slice(CHUNK // 2, CHUNK))
+        APART = STEPS - 1
+        neg_kh = {}
         unit_tiles = {}
         step_tiles = {}
+
+        def tanh(step):
+            cand = step_tiles[step][3]
+            for part in PARTS if step == STEPS - 1 else (slice(0, CHUNK),):
+                nc.scalar.activation(
+                    out=cand[:, part],
+                    in_=cand[:, part],
+                    func=ACT.Tanh,
+                    bias=column(bias, BIH_ROW + 2 * BLOCKS + step // DIRS % BLOCKS),
+                )
 
         def gates(step):
             unit, d = divmod(step, DIRS)
@@ -224,6 +237,8 @@ def tile_graphconvolution_pb_kernel(
             nc.scalar.activation(
                 out=r_gate[:], in_=r_bank[:], func=ACT.Sigmoid, bias=column(r_bias, j)
             )
+            if step == STEPS - 1:
+                tanh(step - 1)
             z_bank = psum.tile([P, CHUNK], F32, tag="gate", bufs=3)
             mx_pass(z_bank, wih_w, Z_COL + j * P, 1 + d, c, True, False)
             mx_pass(z_bank, whh_w, Z_COL + j * P, 0, c, False, True)
@@ -252,8 +267,7 @@ def tile_graphconvolution_pb_kernel(
             j = unit % BLOCKS
             hn_bank, t_gate = unit_tiles[unit]
             in_bank, r_gate, keep, cand = step_tiles[step]
-            parts = (slice(0, CHUNK // 2), slice(CHUNK // 2, CHUNK))
-            for part in parts:
+            for part in PARTS:
                 nc.vector.scalar_tensor_tensor(
                     out=cand[:, part],
                     in0=hn_bank[:, part],
@@ -262,7 +276,7 @@ def tile_graphconvolution_pb_kernel(
                     op0=ALU.add,
                     op1=ALU.mult,
                 )
-            for part in parts:
+            for part in PARTS:
                 nc.vector.tensor_tensor(
                     out=cand[:, part], in0=in_bank[:, part], in1=cand[:, part], op=ALU.add
                 )
@@ -270,22 +284,33 @@ def tile_graphconvolution_pb_kernel(
         def blend(step):
             c, j = divmod(step // DIRS, BLOCKS)
             in_bank, r_gate, keep, cand = step_tiles[step]
-            nc.scalar.activation(
-                out=cand[:], in_=cand[:], func=ACT.Tanh, bias=column(bias, BIH_ROW + 2 * BLOCKS + j)
-            )
+            if step == STEPS - 1:
+                for part in PARTS:
+                    nc.vector.tensor_tensor(
+                        out=cand[:, part], in0=cand[:, part], in1=keep[:, part], op=ALU.mult
+                    )
+                return
             nc.vector.tensor_tensor(
                 out=cand[:], in0=cand[:], in1=x_by_feature[c][:, j, :], op=ALU.subtract
             )
-            helper(step == STEPS - 1).tensor_tensor(
-                out=cand[:], in0=cand[:], in1=keep[:], op=ALU.mult
+            nc.gpsimd.tensor_tensor(out=cand[:], in0=cand[:], in1=keep[:], op=ALU.mult)
+
+        def keep_times_h(step):
+            c, j = divmod(step // DIRS, BLOCKS)
+            keep = step_tiles[step][2]
+            neg_kh[step] = work.tile([P, CHUNK], F32, name="neg_kh")
+            nc.vector.scalar_tensor_tensor(
+                out=neg_kh[step][:],
+                in0=keep[:],
+                scalar=-1.0,
+                in1=x_by_feature[c][:, j, :],
+                op0=ALU.mult,
+                op1=ALU.mult,
             )
 
         back_tiles = {}
 
         HALVES = (slice(0, TILES // 2), slice(TILES // 2, TILES))
-
-        def halves(unit):
-            return HALVES
 
         def finish_back(unit):
             c, j = divmod(unit, BLOCKS)
@@ -296,26 +321,48 @@ def tile_graphconvolution_pb_kernel(
             t_back = psum.tile([P, TILES, P], F32, name="t_back", tag=tag, bufs=bufs)
             for a in range(TILES):
                 nc.tensor.transpose(t_back[:, a, :], t_gate[:, a * P : (a + 1) * P], ident_f32[:])
-            sum_bank = psum.tile([P, TILES, P], F32, name="sum_bank", tag=tag, bufs=bufs)
-            nc.tensor.matmul(sum_bank[:], lhsT=three_ident[:], rhs=x_block, start=True, stop=False)
-            for d in range(DIRS):
-                in_bank, r_gate, keep, cand = step_tiles[unit * DIRS + d]
-                for a in range(TILES):
+            parts = HALVES if last else (slice(0, TILES),)
+            banks = [
+                psum.tile([P, TILES, P], F32, name="sum_bank", tag=tag, bufs=bufs) for part in parts
+            ]
+
+            def add_three_x(start, stop):
+                for part, bank in zip(parts, banks):
                     nc.tensor.matmul(
-                        sum_bank[:, a, :],
-                        lhsT=cand[:, a * P : (a + 1) * P],
-                        rhs=ident_f32[:],
-                        is_transpose=True,
-                        start=False,
-                        stop=(d == DIRS - 1 and a == TILES - 1),
+                        bank[:, part, :],
+                        lhsT=three_ident[:],
+                        rhs=x_block[:, part, :],
+                        start=start,
+                        stop=stop,
                     )
-            back_tiles[unit] = (t_back, sum_bank, work.tile([P, TILES, P], F32, name="result"))
+
+            if last:
+                add_three_x(True, False)
+            addends = []
+            for step in range(unit * DIRS, (unit + 1) * DIRS):
+                addends += [neg_kh[step]] if step in neg_kh else []
+                addends.append(step_tiles[step][3])
+            for tile in addends:
+                for part, bank in zip(parts, banks):
+                    for a in range(part.start, part.stop):
+                        nc.tensor.matmul(
+                            bank[:, a, :],
+                            lhsT=tile[:, a * P : (a + 1) * P],
+                            rhs=ident_f32[:],
+                            is_transpose=True,
+                            start=(not last and tile is addends[0] and a == 0),
+                            stop=(last and tile is addends[-1] and a == part.stop - 1),
+                        )
+            if not last:
+                add_three_x(False, True)
+            halves_of_sum = [(part, banks[i % len(banks)]) for i, part in enumerate(HALVES)]
+            back_tiles[unit] = (t_back, halves_of_sum, work.tile([P, TILES, P], F32, name="result"))
 
         def finish_relu(unit):
             c, j = divmod(unit, BLOCKS)
             x_block = raw[0, c][:, :, j * P : (j + 1) * P]
-            t_back, sum_bank, result = back_tiles[unit]
-            for part in halves(unit):
+            t_back, halves_of_sum, result = back_tiles[unit]
+            for part, sum_bank in halves_of_sum:
                 nc.vector.scalar_tensor_tensor(
                     out=result[:, part, :],
                     in0=sum_bank[:, part, :],
@@ -329,8 +376,8 @@ def tile_graphconvolution_pb_kernel(
             c, j = divmod(unit, BLOCKS)
             feats = slice(j * P, (j + 1) * P)
             x_block = raw[0, c][:, :, feats]
-            t_back, sum_bank, result = back_tiles[unit]
-            for part in halves(unit):
+            t_back, halves_of_sum, result = back_tiles[unit]
+            for part in HALVES:
                 nc.vector.tensor_tensor(
                     out=result[:, part, :], in0=result[:, part, :], in1=t_back[:, part, :], op=ALU.mult
                 )
@@ -357,15 +404,16 @@ def tile_graphconvolution_pb_kernel(
                 gates(tick)
                 candidate(tick)
             if 0 <= tick - 1 < STEPS:
+                if tick - 1 != STEPS - 2:
+                    tanh(tick - 1)
                 blend(tick - 1)
-            if tick == STEPS:
-                finish_rest(STEPS // DIRS - 2)
+            if APART <= tick < STEPS:
+                keep_times_h(tick)
             ended = tick - 1 - BACK_LAG
             if ended >= 0 and ended % DIRS == DIRS - 1:
                 finish_back(ended // DIRS)
                 finish_relu(ended // DIRS)
-                if tick != STEPS - 1:
-                    finish_rest(ended // DIRS)
+                finish_rest(ended // DIRS)
             if tick == 0:
                 transpose_x(0)
             unit, d = divmod(tick, DIRS)

@@ -91,12 +91,11 @@ def tile_graphconvolution_pb_kernel(
         load_gate_codes(wih_codes, wih_words, 0)
         wh_plane = load_scales(wh_scales, "wh")
         nc.sync.dma_start(out=wh_codes[:].bitcast(I32), in_=as_int32(wh_words))
-        for j in range(1, BLOCKS):
-            load_gate_codes(whh_codes, whh_words, j)
-            load_gate_codes(wih_codes, wih_words, j)
-        for c in range(1, CHUNKS):
-            for s in range(1 + DIRS):
-                load_source(s, c)
+        for j in range(BLOCKS):
+            if j > 0:
+                load_gate_codes(whh_codes, whh_words, j)
+                load_gate_codes(wih_codes, wih_words, j)
+            load_source(j, 1)
         whh_w = (whh_codes, whh_plane)
         wih_w = (wih_codes, wih_plane)
         wh_w = (wh_codes, wh_plane)
@@ -227,7 +226,7 @@ def tile_graphconvolution_pb_kernel(
             step_tiles[step] = (
                 psum.tile([P, CHUNK], F32, name="in_bank", tag="in", bufs=2),
                 work.tile([P, CHUNK], F32, name="r_gate"),
-                work.tile([P, CHUNK], F32, name="keep", bufs=4),
+                work.tile([P, CHUNK], F32, name="keep", bufs=6),
                 work.tile([P, CHUNK], F32, name="cand", bufs=DIRS + 2 + BACK_LAG),
             )
             in_bank, r_gate, keep, cand = step_tiles[step]
@@ -290,6 +289,9 @@ def tile_graphconvolution_pb_kernel(
                         out=cand[:, part], in0=cand[:, part], in1=keep[:, part], op=ALU.mult
                     )
                 return
+            if step >= STEPS - DIRS:
+                nc.gpsimd.tensor_tensor(out=cand[:], in0=cand[:], in1=keep[:], op=ALU.mult)
+                return
             nc.vector.tensor_tensor(
                 out=cand[:], in0=cand[:], in1=x_by_feature[c][:, j, :], op=ALU.subtract
             )
@@ -316,47 +318,92 @@ def tile_graphconvolution_pb_kernel(
             c, j = divmod(unit, BLOCKS)
             hn_bank, t_gate = unit_tiles[unit]
             x_block = raw[0, c][:, :, j * P : (j + 1) * P]
-            last = unit == STEPS // DIRS - 1
-            tag, bufs = ("gate", 3) if last else ("back", 2)
-            t_back = psum.tile([P, TILES, P], F32, name="t_back", tag=tag, bufs=bufs)
+            t_back = psum.tile([P, TILES, P], F32, name="t_back", tag="back", bufs=2)
             for a in range(TILES):
                 nc.tensor.transpose(t_back[:, a, :], t_gate[:, a * P : (a + 1) * P], ident_f32[:])
-            parts = HALVES if last else (slice(0, TILES),)
-            banks = [
-                psum.tile([P, TILES, P], F32, name="sum_bank", tag=tag, bufs=bufs) for part in parts
-            ]
-
-            def add_three_x(start, stop):
-                for part, bank in zip(parts, banks):
+            sum_bank = psum.tile([P, TILES, P], F32, name="sum_bank", tag="back", bufs=2)
+            nc.tensor.matmul(sum_bank[:], lhsT=three_ident[:], rhs=x_block, start=True, stop=False)
+            for d in range(DIRS):
+                cand = step_tiles[unit * DIRS + d][3]
+                for a in range(TILES):
                     nc.tensor.matmul(
-                        bank[:, part, :],
-                        lhsT=three_ident[:],
-                        rhs=x_block[:, part, :],
-                        start=start,
-                        stop=stop,
+                        sum_bank[:, a, :],
+                        lhsT=cand[:, a * P : (a + 1) * P],
+                        rhs=ident_f32[:],
+                        is_transpose=True,
+                        start=False,
+                        stop=(d == DIRS - 1 and a == TILES - 1),
+                    )
+            halves_of_sum = [(part, sum_bank) for part in HALVES]
+            back_tiles[unit] = (t_back, halves_of_sum, work.tile([P, TILES, P], F32, name="result"))
+
+        def sum_transposed(bank, part, tiles):
+            for i, tile in enumerate(tiles):
+                for a in range(part.start, part.stop):
+                    nc.tensor.matmul(
+                        bank[:, a, :],
+                        lhsT=tile[:, a * P : (a + 1) * P],
+                        rhs=ident_f32[:],
+                        is_transpose=True,
+                        start=(i == 0 and a == part.start),
+                        stop=(i == len(tiles) - 1 and a == part.stop - 1),
                     )
 
-            if last:
-                add_three_x(True, False)
-            addends = []
-            for step in range(unit * DIRS, (unit + 1) * DIRS):
-                addends += [neg_kh[step]] if step in neg_kh else []
-                addends.append(step_tiles[step][3])
-            for tile in addends:
-                for part, bank in zip(parts, banks):
+        def last_t():
+            unit = STEPS // DIRS - 1
+            t_gate = unit_tiles[unit][1]
+            c, j = divmod(unit, BLOCKS)
+            x_block = raw[0, c][:, :, j * P : (j + 1) * P]
+            t_back = psum.tile([P, TILES, P], F32, name="t_back", tag="gate", bufs=3)
+            for a in range(TILES):
+                nc.tensor.transpose(t_back[:, a, :], t_gate[:, a * P : (a + 1) * P], ident_f32[:])
+            carry = work.tile([P, TILES, P], F32, name="carry")
+            nc.vector.scalar_tensor_tensor(
+                out=carry[:], in0=t_back[:], scalar=1.0, in1=x_block, op0=ALU.subtract, op1=ALU.mult
+            )
+            keep_bank = psum.tile([P, TILES, P], F32, name="keep_bank", tag="gate", bufs=3)
+            sum_transposed(keep_bank, slice(0, TILES), [step_tiles[unit * DIRS + d][2] for d in range(DIRS)])
+            neg_zh = work.tile([P, TILES, P], F32, name="neg_zh")
+            nc.vector.scalar_tensor_tensor(
+                out=neg_zh[:], in0=keep_bank[:], scalar=3.0, in1=x_block, op0=ALU.subtract, op1=ALU.mult
+            )
+            back_tiles["last"] = (t_back, carry, neg_zh)
+
+        def last_rest():
+            unit = STEPS // DIRS - 1
+            c, j = divmod(unit, BLOCKS)
+            feats = slice(j * P, (j + 1) * P)
+            t_back, carry, neg_zh = back_tiles["last"]
+            banks = [
+                psum.tile([P, TILES, P], F32, name="sum_a", tag="gate", bufs=3),
+                psum.tile([P, TILES, P], F32, name="sum_b", tag="in", bufs=2),
+            ]
+            result = work.tile([P, TILES, P], F32, name="result")
+            for d in range(DIRS):
+                for part, bank in zip(HALVES, banks):
+                    cand = step_tiles[unit * DIRS + d][3]
                     for a in range(part.start, part.stop):
                         nc.tensor.matmul(
                             bank[:, a, :],
-                            lhsT=tile[:, a * P : (a + 1) * P],
+                            lhsT=cand[:, a * P : (a + 1) * P],
                             rhs=ident_f32[:],
                             is_transpose=True,
-                            start=(not last and tile is addends[0] and a == 0),
-                            stop=(last and tile is addends[-1] and a == part.stop - 1),
+                            start=(d == 0 and a == part.start),
+                            stop=(d == DIRS - 1 and a == part.stop - 1),
                         )
-            if not last:
-                add_three_x(False, True)
-            halves_of_sum = [(part, banks[i % len(banks)]) for i, part in enumerate(HALVES)]
-            back_tiles[unit] = (t_back, halves_of_sum, work.tile([P, TILES, P], F32, name="result"))
+            for part, bank in zip(HALVES, banks):
+                nc.vector.tensor_tensor(
+                    out=result[:, part, :], in0=bank[:, part, :], in1=neg_zh[:, part, :], op=ALU.subtract
+                )
+            for part in HALVES:
+                nc.vector.scalar_tensor_tensor(
+                    out=result[:, part, :], in0=result[:, part, :], scalar=0.0, in1=t_back[:, part, :], op0=ALU.max, op1=ALU.mult
+                )
+            for part in HALVES:
+                nc.vector.tensor_tensor(
+                    out=result[:, part, :], in0=result[:, part, :], in1=carry[:, part, :], op=ALU.subtract
+                )
+                nc.sync.dma_start(out=out_rows[c][:, part, feats], in_=result[:, part, :])
 
         def finish_relu(unit):
             c, j = divmod(unit, BLOCKS)
@@ -403,17 +450,22 @@ def tile_graphconvolution_pb_kernel(
             if tick < STEPS:
                 gates(tick)
                 candidate(tick)
+            if tick == STEPS:
+                last_t()
             if 0 <= tick - 1 < STEPS:
                 if tick - 1 != STEPS - 2:
                     tanh(tick - 1)
                 blend(tick - 1)
-            if APART <= tick < STEPS:
-                keep_times_h(tick)
+            if tick == STEPS:
+                finish_rest(STEPS // DIRS - 2)
             ended = tick - 1 - BACK_LAG
-            if ended >= 0 and ended % DIRS == DIRS - 1:
+            if ended == STEPS - 1:
+                last_rest()
+            elif ended >= 0 and ended % DIRS == DIRS - 1:
                 finish_back(ended // DIRS)
                 finish_relu(ended // DIRS)
-                finish_rest(ended // DIRS)
+                if tick != STEPS - 1:
+                    finish_rest(ended // DIRS)
             if tick == 0:
                 transpose_x(0)
             unit, d = divmod(tick, DIRS)

@@ -53,10 +53,11 @@ def tile_graphconvolution_pb_kernel(
 
         def load_source(s, c):
             raw[s, c] = const.tile([P, TILES, FEAT], BF16, name="raw%d_%d" % (s, c))
-            nc.sync.dma_start(
-                out=raw[s, c][:],
-                in_=sources[s].rearrange("(c p a) k -> c p a k", p=P, a=TILES)[c],
-            )
+            for part in ((slice(0, 2), slice(2, 4)) if (s, c) == (0, 0) else (slice(0, 4),)):
+                nc.sync.dma_start(
+                    out=raw[s, c][:, part, :],
+                    in_=sources[s].rearrange("(c p a) k -> c p a k", p=P, a=TILES)[c][:, part, :],
+                )
 
         def load_scales(scales, label):
             plane = const.tile([P, scales.shape[2]], U8, name=label + "_plane", align_bytes=64)
@@ -78,17 +79,17 @@ def tile_graphconvolution_pb_kernel(
                 in_=as_int32(words).rearrange(by_block, g=GATES, j=BLOCKS)[:, :, j, :],
             )
 
-        load_source(0, 0)
-        load_source(1, 0)
-        whh_plane = load_scales(whh_scales, "whh")
-        load_source(2, 0)
-        load_source(3, 0)
-        wih_plane = load_scales(wih_scales, "wih")
         whh_codes = const.tile([P, 4 * GATES * FEAT], U8, align_bytes=64)
         wih_codes = const.tile([P, 4 * GATES * FEAT], U8, align_bytes=64)
         wh_codes = const.tile([P, 4 * FEAT], U8, align_bytes=64)
+        load_source(0, 0)
+        whh_plane = load_scales(whh_scales, "whh")
+        load_source(1, 0)
+        load_source(2, 0)
+        wih_plane = load_scales(wih_scales, "wih")
         load_gate_codes(whh_codes, whh_words, 0)
         load_gate_codes(wih_codes, wih_words, 0)
+        load_source(3, 0)
         wh_plane = load_scales(wh_scales, "wh")
         nc.sync.dma_start(out=wh_codes[:].bitcast(I32), in_=as_int32(wh_words))
         for j in range(BLOCKS):
@@ -111,10 +112,10 @@ def tile_graphconvolution_pb_kernel(
                 out=bias_rows[first_row : first_row + as_rows.shape[0], :], in_=as_rows
             )
         ident_bf = const.tile([P, P], BF16)
-        make_identity(nc, ident_bf[:])
+        nc.vector.tensor_copy(out=ident_bf[:], in_=ident_f32[:])
         three_ident = const.tile([P, P], BF16)
         nc.vector.tensor_scalar(
-            out=three_ident[:], in0=ident_bf[:], scalar1=3.0, scalar2=None, op0=ALU.mult
+            out=three_ident[:], in0=ident_f32[:], scalar1=3.0, scalar2=None, op0=ALU.mult
         )
 
         bias = const.tile([P, P], F32)
@@ -434,15 +435,13 @@ def tile_graphconvolution_pb_kernel(
                 )
                 nc.sync.dma_start(out=out_rows[c][:, part, feats], in_=result[:, part, :])
 
-        for s in range(1 + DIRS):
+        for s in range(DIRS):
             transpose_source(s, 0)
             if s > 0:
                 quantise_source(s - 1, 0)
-            if s == DIRS:
-                spread_biases()
-        quantise_source(DIRS, 0)
-
-        transposed = []
+        spread_biases()
+        transpose_x(0)
+        transposed = [(DIRS - 1, 0)]
         for tick in range(STEPS + 1 + BACK_LAG):
             for s, c in transposed:
                 quantise_source(s, c)
@@ -467,10 +466,11 @@ def tile_graphconvolution_pb_kernel(
                 if tick != STEPS - 1:
                     finish_rest(ended // DIRS)
             if tick == 0:
-                transpose_x(0)
+                transpose_source(DIRS, 0)
+                transposed = [(DIRS, 0)]
             unit, d = divmod(tick, DIRS)
             c, j = divmod(unit, BLOCKS)
-            if d == DIRS - 1 and unit + 1 < STEPS // DIRS:
+            if d == DIRS - 1 and unit + 2 < STEPS // DIRS:
                 transpose_x(unit + 1)
             if c + 1 < CHUNKS and d == DIRS - 1:
                 transpose_source(j, c + 1)

@@ -240,8 +240,8 @@ def tile_graphconvolution_pb_kernel(
             if step == STEPS - 1:
                 tanh(step - 1)
             z_bank = psum.tile([P, CHUNK], F32, tag="gate", bufs=3)
-            mx_pass(z_bank, wih_w, Z_COL + j * P, 1 + d, c, True, False)
-            mx_pass(z_bank, whh_w, Z_COL + j * P, 0, c, False, True)
+            mx_pass(z_bank, whh_w, Z_COL + j * P, 0, c, True, False)
+            mx_pass(z_bank, wih_w, Z_COL + j * P, 1 + d, c, False, True)
             nc.scalar.activation(
                 out=keep[:],
                 in_=z_bank[:],

@@ -53,11 +53,10 @@ def tile_graphconvolution_pb_kernel(
 
         def load_source(s, c):
             raw[s, c] = const.tile([P, TILES, FEAT], BF16, name="raw%d_%d" % (s, c))
-            for part in ((slice(0, 2), slice(2, 4)) if (s, c) == (0, 0) else (slice(0, 4),)):
-                nc.sync.dma_start(
-                    out=raw[s, c][:, part, :],
-                    in_=sources[s].rearrange("(c p a) k -> c p a k", p=P, a=TILES)[c][:, part, :],
-                )
+            nc.sync.dma_start(
+                out=raw[s, c][:],
+                in_=sources[s].rearrange("(c p a) k -> c p a k", p=P, a=TILES)[c],
+            )
 
         def load_scales(scales, label):
             plane = const.tile([P, scales.shape[2]], U8, name=label + "_plane", align_bytes=64)
@@ -86,9 +85,9 @@ def tile_graphconvolution_pb_kernel(
         whh_plane = load_scales(whh_scales, "whh")
         load_source(1, 0)
         load_source(2, 0)
-        wih_plane = load_scales(wih_scales, "wih")
         load_gate_codes(whh_codes, whh_words, 0)
         load_gate_codes(wih_codes, wih_words, 0)
+        wih_plane = load_scales(wih_scales, "wih")
         load_source(3, 0)
         wh_plane = load_scales(wh_scales, "wh")
         nc.sync.dma_start(out=wh_codes[:].bitcast(I32), in_=as_int32(wh_words))

from contextlib import ExitStack

import concourse.mybir as mybir
from concourse.masks import make_identity

F32 = mybir.dt.float32
BF16 = mybir.dt.bfloat16
I32 = mybir.dt.int32
U32 = mybir.dt.uint32
U8 = mybir.dt.uint8
FP8X4 = mybir.dt.float8_e4m3fn_x4
ACT = mybir.ActivationFunctionType
ALU = mybir.AluOpType

P = 128
DIRS = 3
NODES = 1024
FEAT = 512
GATES = 3
CHUNK = 512
TILES = CHUNK // P
CHUNKS = NODES // CHUNK
BLOCKS = FEAT // P
STEPS = CHUNKS * BLOCKS * DIRS
R_COL = 0
Z_COL = FEAT
N_COL = 2 * FEAT
BIH_ROW = 0
BHH_ROW = GATES * BLOCKS
BH_ROW = 2 * GATES * BLOCKS
BACK_LAG = 2

FLOPS = 2 * FEAT * NODES * (DIRS * GATES * FEAT + GATES * FEAT + FEAT)


def tile_graphconvolution_pb_kernel(
    tc, agg, x, wih_words, wih_scales, whh_words, whh_scales, bih, bhh, wh_words, wh_scales, bh, out
):
    nc = tc.nc
    with ExitStack() as ctx:
        ctx.enter_context(tc.manual_schedule())
        const = ctx.enter_context(tc.tile_pool(name="const", bufs=1))
        stage = ctx.enter_context(tc.tile_pool(name="stage", bufs=3))
        work = ctx.enter_context(tc.tile_pool(name="work", bufs=3))
        psum = ctx.enter_context(tc.psum_pool(name="psum", bufs=1))

        warm = const.tile([P, 1], F32)
        nc.vector.memset(warm[:], 0.0)
        nc.scalar.activation(out=warm[:], in_=warm[:], func=ACT.Sigmoid)

        sources = [x[:, 0, :]] + [agg[d, 0] for d in range(DIRS)]
        raw = {}

        def load_source(s, c):
            raw[s, c] = const.tile([P, TILES, FEAT], BF16, name="raw%d_%d" % (s, c))
            nc.sync.dma_start(
                out=raw[s, c][:],
                in_=sources[s].rearrange("(c p a) k -> c p a k", p=P, a=TILES)[c],
            )

        def load_scales(scales, label):
            plane = const.tile([P, scales.shape[2]], U8, name=label + "_plane", align_bytes=64)
            nc.vector.memset(plane[:].bitcast(I32), 0)
            for quad in range(4):
                nc.sync.dma_start(
                    out=plane[32 * quad : 32 * quad + 4, :].bitcast(I32),
                    in_=scales[0, 4 * quad : 4 * quad + 4, :].bitcast(I32),
                )
            return plane

        def as_int32(words):
            return words[0].rearrange("p n t -> p (n t)").bitcast(I32)

        def load_gate_codes(codes, words, j):
            by_block = "p (g j n) -> p g j n"
            nc.sync.dma_start(
                out=codes[:].bitcast(I32).rearrange(by_block, g=GATES, j=BLOCKS)[:, :, j, :],
                in_=as_int32(words).rearrange(by_block, g=GATES, j=BLOCKS)[:, :, j, :],
            )

        whh_codes = const.tile([P, 4 * GATES * FEAT], U8, align_bytes=64)
        wih_codes = const.tile([P, 4 * GATES * FEAT], U8, align_bytes=64)
        wh_codes = const.tile([P, 4 * FEAT], U8, align_bytes=64)
        load_source(0, 0)
        whh_plane = load_scales(whh_scales, "whh")
        load_source(1, 0)
        load_source(2, 0)
        load_gate_codes(whh_codes, whh_words, 0)
        load_gate_codes(wih_codes, wih_words, 0)
        wih_plane = load_scales(wih_scales, "wih")
        load_source(3, 0)
        wh_plane = load_scales(wh_scales, "wh")
        nc.sync.dma_start(out=wh_codes[:].bitcast(I32), in_=as_int32(wh_words))
        for j in range(BLOCKS):
            if j > 0:
                load_gate_codes(whh_codes, whh_words, j)
                load_gate_codes(wih_codes, wih_words, j)
            load_source(j, 1)
        whh_w = (whh_codes, whh_plane)
        wih_w = (wih_codes, wih_plane)
        wh_w = (wh_codes, wh_plane)
        out_rows = out[:, 0, :].rearrange("(c p a) f -> c p a f", p=P, a=TILES)

        ident_f32 = const.tile([P, P], F32)
        make_identity(nc, ident_f32[:])
        bias_rows = const.tile([P, P], BF16)
        nc.vector.memset(bias_rows[:], 0.0)
        for first_row, vector in ((BIH_ROW, bih), (BHH_ROW, bhh), (BH_ROW, bh)):
            as_rows = vector.rearrange("(r f) -> r f", f=P)
            nc.gpsimd.dma_start(
                out=bias_rows[first_row : first_row + as_rows.shape[0], :], in_=as_rows
            )
        ident_bf = const.tile([P, P], BF16)
        nc.vector.tensor_copy(out=ident_bf[:], in_=ident_f32[:])
        three_ident = const.tile([P, P], BF16)
        nc.vector.tensor_scalar(
            out=three_ident[:], in0=ident_f32[:], scalar1=3.0, scalar2=None, op0=ALU.mult
        )

        bias = const.tile([P, P], F32)
        r_bias = const.tile([P, BLOCKS], F32)
        neg_z_bias = const.tile([P, BLOCKS], F32)

        def spread_biases():
            bias_bank = psum.tile([P, P], BF16, tag="gate", bufs=3)
            nc.tensor.transpose(bias_bank[:], bias_rows[:], ident_bf[:])
            nc.vector.tensor_copy(out=bias[:], in_=bias_bank[:])
            nc.vector.tensor_tensor(
                out=r_bias[:],
                in0=bias[:, BIH_ROW : BIH_ROW + BLOCKS],
                in1=bias[:, BHH_ROW : BHH_ROW + BLOCKS],
                op=ALU.add,
            )
            nc.vector.scalar_tensor_tensor(
                out=neg_z_bias[:],
                in0=bias[:, BIH_ROW + BLOCKS : BIH_ROW + 2 * BLOCKS],
                scalar=-1.0,
                in1=bias[:, BHH_ROW + BLOCKS : BHH_ROW + 2 * BLOCKS],
                op0=ALU.mult,
                op1=ALU.subtract,
            )

        def column(table, i):
            return table[:, i : i + 1]

        grouped = {}
        quantised = {}
        x_by_feature = {}

        def transpose_source(s, c):
            pairs = raw[s, c][:].rearrange("p a k -> p (a k)").bitcast(F32)
            grouped[s, c] = stage.tile([P, 4 * CHUNK], BF16, name="grouped", align_bytes=64)
            grouped_pairs = grouped[s, c][:].bitcast(F32).rearrange("p (m u) -> p m u", u=2)
            for half in range(2):
                bank = psum.tile([P, 2, 2 * P], F32, tag="gate", bufs=3)
                for a in (2 * half, 2 * half + 1):
                    first = a * FEAT // 2
                    for u in range(2):
                        nc.tensor.transpose(
                            bank[:, u, (a % 2) * P : (a % 2 + 1) * P],
                            pairs[:, first + u : first + FEAT // 2 : 2],
                            ident_f32[:],
                        )
                nc.scalar.copy(
                    out=grouped_pairs[:, 2 * P * half : 2 * P * (half + 1), :],
                    in_=bank[:].rearrange("p u m -> p m u"),
                )

        def transpose_x(unit):
            c, j = divmod(unit, BLOCKS)
            if j == 0:
                x_by_feature[c] = const.tile([P, BLOCKS, CHUNK], BF16, name="xT%d" % c)
            bank = psum.tile([P, CHUNK], BF16, tag="gate", bufs=3)
            for a in range(TILES):
                nc.tensor.transpose(
                    bank[:, a * P : (a + 1) * P], raw[0, c][:, a, j * P : (j + 1) * P], ident_bf[:]
                )
            nc.scalar.copy(out=x_by_feature[c][:, j, :], in_=bank[:])

        def quantise_source(s, c):
            codes = const.tile([P, CHUNK], U32, name="codes%d_%d" % (s, c), align_bytes=64)
            plane = const.tile([P, CHUNK], U8, name="plane%d_%d" % (s, c), align_bytes=64)
            nc.vector.quantize_mx(
                out=codes[:].bitcast(FP8X4), scales=plane[:], in_=grouped[s, c][:]
            )
            quantised[s, c] = (codes, plane)

        def mx_pass(bank, weight, first_col, s, c, start, stop):
            w_codes, w_plane = weight
            a_codes, a_plane = quantised[s, c]
            nc.tensor.matmul_mx(
                out=bank[:],
                lhsT=w_codes[:, 4 * first_col : 4 * (first_col + P)].bitcast(FP8X4),
                lhsT_scale=w_plane[:, first_col : first_col + P],
                rhs=a_codes[:].bitcast(FP8X4),
                rhs_scale=a_plane[:],
                start=start,
                stop=stop,
            )

        PARTS = (slice(0, CHUNK // 2), slice(CHUNK // 2, CHUNK))
        APART = STEPS - 1
        neg_kh = {}
        unit_tiles = {}
        step_tiles = {}

        def tanh(step):
            cand = step_tiles[step][3]
            for part in PARTS if step == STEPS - 1 else (slice(0, CHUNK),):
                nc.scalar.activation(
                    out=cand[:, part],
                    in_=cand[:, part],
                    func=ACT.Tanh,
                    bias=column(bias, BIH_ROW + 2 * BLOCKS + step // DIRS % BLOCKS),
                )

        def gates(step):
            unit, d = divmod(step, DIRS)
            c, j = divmod(unit, BLOCKS)
            if d == 0:
                unit_tiles[unit] = (
                    psum.tile([P, CHUNK], F32, name="hn_bank", tag="hn", bufs=1),
                    work.tile([P, CHUNK], F32, name="t_gate"),
                )
            hn_bank, t_gate = unit_tiles[unit]
            step_tiles[step] = (
                psum.tile([P, CHUNK], F32, name="in_bank", tag="in", bufs=2),
                work.tile([P, CHUNK], F32, name="r_gate"),
                work.tile([P, CHUNK], F32, name="keep", bufs=6),
                work.tile([P, CHUNK], F32, name="cand", bufs=DIRS + 2 + BACK_LAG),
            )
            in_bank, r_gate, keep, cand = step_tiles[step]
            r_bank = psum.tile([P, CHUNK], F32, tag="gate", bufs=3)
            mx_pass(r_bank, wih_w, R_COL + j * P, 1 + d, c, True, False)
            mx_pass(r_bank, whh_w, R_COL + j * P, 0, c, False, True)
            nc.scalar.activation(
                out=r_gate[:], in_=r_bank[:], func=ACT.Sigmoid, bias=column(r_bias, j)
            )
            if step == STEPS - 1:
                tanh(step - 1)
            z_bank = psum.tile([P, CHUNK], F32, tag="gate", bufs=3)
            mx_pass(z_bank, whh_w, Z_COL + j * P, 0, c, True, False)
            mx_pass(z_bank, wih_w, Z_COL + j * P, 1 + d, c, False, True)
            nc.scalar.activation(
                out=keep[:],
                in_=z_bank[:],
                func=ACT.Sigmoid,
                bias=column(neg_z_bias, j),
                scale=-1.0,
            )
            if d == 0:
                mx_pass(hn_bank, whh_w, N_COL + j * P, 0, c, True, True)
            mx_pass(in_bank, wih_w, N_COL + j * P, 1 + d, c, True, True)
            if d == 1:
                t_bank = psum.tile([P, CHUNK], F32, tag="gate", bufs=3)
                mx_pass(t_bank, wh_w, j * P, 0, c, True, True)
                nc.scalar.activation(
                    out=t_gate[:], in_=t_bank[:], func=ACT.Relu, bias=column(bias, BH_ROW + j)
                )

        def helper(at_the_end):
            return nc.vector if at_the_end else nc.gpsimd

        def candidate(step):
            unit = step // DIRS
            j = unit % BLOCKS
            hn_bank, t_gate = unit_tiles[unit]
            in_bank, r_gate, keep, cand = step_tiles[step]
            for part in PARTS:
                nc.vector.scalar_tensor_tensor(
                    out=cand[:, part],
                    in0=hn_bank[:, part],
                    scalar=column(bias, BHH_ROW + 2 * BLOCKS + j),
                    in1=r_gate[:, part],
                    op0=ALU.add,
                    op1=ALU.mult,
                )
            for part in PARTS:
                nc.vector.tensor_tensor(
                    out=cand[:, part], in0=in_bank[:, part], in1=cand[:, part], op=ALU.add
                )

        def blend(step):
            c, j = divmod(step // DIRS, BLOCKS)
            in_bank, r_gate, keep, cand = step_tiles[step]
            if step == STEPS - 1:
                for part in PARTS:
                    nc.vector.tensor_tensor(
                        out=cand[:, part], in0=cand[:, part], in1=keep[:, part], op=ALU.mult
                    )
                return
            if step >= STEPS - DIRS:
                nc.gpsimd.tensor_tensor(out=cand[:], in0=cand[:], in1=keep[:], op=ALU.mult)
                return
            nc.vector.tensor_tensor(
                out=cand[:], in0=cand[:], in1=x_by_feature[c][:, j, :], op=ALU.subtract
            )
            nc.gpsimd.tensor_tensor(out=cand[:], in0=cand[:], in1=keep[:], op=ALU.mult)

        def keep_times_h(step):
            c, j = divmod(step // DIRS, BLOCKS)
            keep = step_tiles[step][2]
            neg_kh[step] = work.tile([P, CHUNK], F32, name="neg_kh")
            nc.vector.scalar_tensor_tensor(
                out=neg_kh[step][:],
                in0=keep[:],
                scalar=-1.0,
                in1=x_by_feature[c][:, j, :],
                op0=ALU.mult,
                op1=ALU.mult,
            )

        back_tiles = {}

        HALVES = (slice(0, TILES // 2), slice(TILES // 2, TILES))

        def finish_back(unit):
            c, j = divmod(unit, BLOCKS)
            hn_bank, t_gate = unit_tiles[unit]
            x_block = raw[0, c][:, :, j * P : (j + 1) * P]
            t_back = psum.tile([P, TILES, P], F32, name="t_back", tag="back", bufs=2)
            for a in range(TILES):
                nc.tensor.transpose(t_back[:, a, :], t_gate[:, a * P : (a + 1) * P], ident_f32[:])
            sum_bank = psum.tile([P, TILES, P], F32, name="sum_bank", tag="back", bufs=2)
            nc.tensor.matmul(sum_bank[:], lhsT=three_ident[:], rhs=x_block, start=True, stop=False)
            for d in range(DIRS):
                cand = step_tiles[unit * DIRS + d][3]
                for a in range(TILES):
                    nc.tensor.matmul(
                        sum_bank[:, a, :],
                        lhsT=cand[:, a * P : (a + 1) * P],
                        rhs=ident_f32[:],
                        is_transpose=True,
                        start=False,
                        stop=(d == DIRS - 1 and a == TILES - 1),
                    )
            halves_of_sum = [(part, sum_bank) for part in HALVES]
            back_tiles[unit] = (t_back, halves_of_sum, work.tile([P, TILES, P], F32, name="result"))

        def sum_transposed(bank, part, tiles):
            for i, tile in enumerate(tiles):
                for a in range(part.start, part.stop):
                    nc.tensor.matmul(
                        bank[:, a, :],
                        lhsT=tile[:, a * P : (a + 1) * P],
                        rhs=ident_f32[:],
                        is_transpose=True,
                        start=(i == 0 and a == part.start),
                        stop=(i == len(tiles) - 1 and a == part.stop - 1),
                    )

        def last_t():
            unit = STEPS // DIRS - 1
            t_gate = unit_tiles[unit][1]
            c, j = divmod(unit, BLOCKS)
            x_block = raw[0, c][:, :, j * P : (j + 1) * P]
            t_back = psum.tile([P, TILES, P], F32, name="t_back", tag="gate", bufs=3)
            for a in range(TILES):
                nc.tensor.transpose(t_back[:, a, :], t_gate[:, a * P : (a + 1) * P], ident_f32[:])
            carry = work.tile([P, TILES, P], F32, name="carry")
            nc.vector.scalar_tensor_tensor(
                out=carry[:], in0=t_back[:], scalar=1.0, in1=x_block, op0=ALU.subtract, op1=ALU.mult
            )
            keep_bank = psum.tile([P, TILES, P], F32, name="keep_bank", tag="gate", bufs=3)
            sum_transposed(keep_bank, slice(0, TILES), [step_tiles[unit * DIRS + d][2] for d in range(DIRS)])
            neg_zh = work.tile([P, TILES, P], F32, name="neg_zh")
            nc.vector.scalar_tensor_tensor(
                out=neg_zh[:], in0=keep_bank[:], scalar=3.0, in1=x_block, op0=ALU.subtract, op1=ALU.mult
            )
            back_tiles["last"] = (t_back, carry, neg_zh)

        def last_rest():
            unit = STEPS // DIRS - 1
            c, j = divmod(unit, BLOCKS)
            feats = slice(j * P, (j + 1) * P)
            t_back, carry, neg_zh = back_tiles["last"]
            banks = [
                psum.tile([P, TILES, P], F32, name="sum_a", tag="gate", bufs=3),
                psum.tile([P, TILES, P], F32, name="sum_b", tag="in", bufs=2),
            ]
            result = work.tile([P, TILES, P], F32, name="result")
            for d in range(DIRS):
                for part, bank in zip(HALVES, banks):
                    cand = step_tiles[unit * DIRS + d][3]
                    for a in range(part.start, part.stop):
                        nc.tensor.matmul(
                            bank[:, a, :],
                            lhsT=cand[:, a * P : (a + 1) * P],
                            rhs=ident_f32[:],
                            is_transpose=True,
                            start=(d == 0 and a == part.start),
                            stop=(d == DIRS - 1 and a == part.stop - 1),
                        )
            for part, bank in zip(HALVES, banks):
                nc.vector.tensor_tensor(
                    out=result[:, part, :], in0=bank[:, part, :], in1=neg_zh[:, part, :], op=ALU.subtract
                )
            for part in HALVES:
                nc.vector.scalar_tensor_tensor(
                    out=result[:, part, :], in0=result[:, part, :], scalar=0.0, in1=t_back[:, part, :], op0=ALU.max, op1=ALU.mult
                )
            for part in HALVES:
                nc.vector.tensor_tensor(
                    out=result[:, part, :], in0=result[:, part, :], in1=carry[:, part, :], op=ALU.subtract
                )
                nc.sync.dma_start(out=out_rows[c][:, part, feats], in_=result[:, part, :])

        def finish_relu(unit):
            c, j = divmod(unit, BLOCKS)
            x_block = raw[0, c][:, :, j * P : (j + 1) * P]
            t_back, halves_of_sum, result = back_tiles[unit]
            for part, sum_bank in halves_of_sum:
                nc.vector.scalar_tensor_tensor(
                    out=result[:, part, :],
                    in0=sum_bank[:, part, :],
                    scalar=0.0,
                    in1=x_block[:, part, :],
                    op0=ALU.max,
                    op1=ALU.subtract,
                )

        def finish_rest(unit):
            c, j = divmod(unit, BLOCKS)
            feats = slice(j * P, (j + 1) * P)
            x_block = raw[0, c][:, :, feats]
            t_back, halves_of_sum, result = back_tiles[unit]
            for part in HALVES:
                nc.vector.tensor_tensor(
                    out=result[:, part, :], in0=result[:, part, :], in1=t_back[:, part, :], op=ALU.mult
                )
            for part in HALVES if unit == STEPS // DIRS - 1 else (slice(0, TILES),):
                helper(unit == STEPS // DIRS - 1).tensor_tensor(
                    out=result[:, part, :], in0=result[:, part, :], in1=x_block[:, part, :], op=ALU.add
                )
                nc.sync.dma_start(out=out_rows[c][:, part, feats], in_=result[:, part, :])

        for s in range(DIRS):
            transpose_source(s, 0)
            if s > 0:
                quantise_source(s - 1, 0)
        spread_biases()
        transpose_x(0)
        transposed = [(DIRS - 1, 0)]
        for tick in range(STEPS + 1 + BACK_LAG):
            for s, c in transposed:
                quantise_source(s, c)
            transposed = []
            if tick < STEPS:
                gates(tick)
                candidate(tick)
            if tick == STEPS:
                last_t()
            if 0 <= tick - 1 < STEPS:
                if tick - 1 != STEPS - 2:
                    tanh(tick - 1)
                blend(tick - 1)
            if tick == STEPS:
                finish_rest(STEPS // DIRS - 2)
            ended = tick - 1 - BACK_LAG
            if ended == STEPS - 1:
                last_rest()
            elif ended >= 0 and ended % DIRS == DIRS - 1:
                finish_back(ended // DIRS)
                finish_relu(ended // DIRS)
                if tick != STEPS - 1:
                    finish_rest(ended // DIRS)
            if tick == 0:
                transpose_source(DIRS, 0)
                transposed = [(DIRS, 0)]
            unit, d = divmod(tick, DIRS)
            c, j = divmod(unit, BLOCKS)
            if d == DIRS - 1 and unit + 2 < STEPS // DIRS:
                transpose_x(unit + 1)
            if c + 1 < CHUNKS and d == DIRS - 1:
                transpose_source(j, c + 1)
                transposed = [(j, c + 1)]
